import numpy as np
import ml_dtypes

BF16 = ml_dtypes.bfloat16


def bf(x):
    return np.asarray(x, np.float32).astype(BF16)


def f32(x):
    return np.asarray(x, np.float32)


def f64(x):
    return np.asarray(x).astype(np.float64)


def striped(idx):
    return np.tile(idx.reshape(-1, 16).T, (8, 1))


C, S, N, LOG2N, L_IN, L_OUT = 512, 2048, 512, 9, 2, 1
A_MAX = 3.0


def strides():
    return [1 << (l % LOG2N) for l in range(L_IN)] + [1 << ((L_OUT - 1 - k) % LOG2N) for k in range(L_OUT)]


def setup_inputs():
    return {"base": f32(np.random.standard_normal((C, S))), "data": f32(np.random.standard_normal((C, N))), "angles": f32(np.random.uniform(-A_MAX, A_MAX, (L_IN + L_OUT, N // 2))), "offs": striped(np.random.permutation(S)[:N])}


def reference(base, data, angles, offs):
    idx = offs[:16].T.reshape(-1)
    y = f64(data)
    ang = f64(angles)
    for l, s in enumerate(strides()):
        nblk = N // (2 * s)
        yr = y.reshape(C, nblk, 2, s)
        a, b = yr[:, :, 0, :], yr[:, :, 1, :]
        cs = np.cos(ang[l]).reshape(nblk, s)
        sn = np.sin(ang[l]).reshape(nblk, s)
        y = np.stack([a * cs - b * sn, a * sn + b * cs], axis=2).reshape(C, N)
    res = f64(base).copy()
    res[:, idx] = y
    return res

@@ -1,0 +1,78 @@
+import math
+
+import concourse.mybir as mybir
+
+F32 = mybir.dt.float32
+U16 = mybir.dt.uint16
+MULT = mybir.AluOpType.mult
+ADD = mybir.AluOpType.add
+SIN = mybir.ActivationFunctionType.Sin
+ABS = mybir.ActivationFunctionType.Abs
+
+P = 128
+ROWS, WIDE, N = 512, 2048, 512
+PAIRS = N // 2
+STRIDES = (1, 2, 1)
+LAYERS = len(STRIDES)
+FLOPS = LAYERS * ROWS * PAIRS * 6
+
+
+def tile_butterflymodule_kernel(tc, base, data, angles, offs, out):
+    nc = tc.nc
+    with (
+        tc.tile_pool(name="held", bufs=1) as held,
+        tc.tile_pool(name="rows", bufs=ROWS // P) as rows,
+        tc.tile_pool(name="work", bufs=2) as work,
+    ):
+        offsets = held.tile([P, N // 16], U16, name="offsets")
+        nc.sync.dma_start(offsets[:], offs)
+
+        angle = held.tile([P, LAYERS, PAIRS], F32, name="angle")
+        nc.sync.dma_start(
+            angle[:].rearrange("k l q -> k (l q)"),
+            angles.rearrange("l q -> (l q)").partition_broadcast(P),
+        )
+
+        windows, fresh = [], []
+        for r in range(ROWS // P):
+            fresh.append(rows.tile([P, N], F32, name="fresh"))
+            nc.sync.dma_start(fresh[r][:], data[r * P : (r + 1) * P, :])
+            windows.append(rows.tile([P, WIDE], F32, name="window"))
+            nc.sync.dma_start(windows[r][:], base[r * P : (r + 1) * P, :])
+
+        size = held.tile([P, LAYERS, PAIRS], F32, name="size")
+        cos = held.tile([P, LAYERS, PAIRS], F32, name="cos")
+        sin = held.tile([P, LAYERS, PAIRS], F32, name="sin")
+        minus_sin = held.tile([P, LAYERS, PAIRS], F32, name="minus_sin")
+        nc.scalar.activation(size[:], angle[:], ABS)
+        nc.scalar.activation(cos[:], size[:], SIN, bias=math.pi / 2, scale=-1.0)
+        nc.scalar.activation(sin[:], angle[:], SIN)
+        nc.scalar.activation(minus_sin[:], angle[:], SIN, scale=-1.0)
+
+        def two_products(y, layer):
+            s = STRIDES[layer]
+
+            def members(columns):
+                return columns.rearrange("k (g e s) -> k g e s", e=2, s=s)
+
+            def per_pair(values):
+                return values[:, layer].rearrange("k (g s) -> k g s", s=s)
+
+            own = work.tile([P, N], F32, name="own")
+            other = work.tile([P, N], F32, name="other")
+            for_both = per_pair(cos).unsqueeze(2).broadcast_to([P, PAIRS // s, 2, s])
+            nc.vector.tensor_tensor(members(own[:]), members(y), for_both, MULT)
+            nc.vector.tensor_tensor(members(other[:])[:, :, 0], members(y)[:, :, 1], per_pair(minus_sin), MULT)
+            nc.vector.tensor_tensor(members(other[:])[:, :, 1], members(y)[:, :, 0], per_pair(sin), MULT)
+            return own, other
+
+        for r in range(ROWS // P):
+            y = fresh[r]
+            for layer in range(LAYERS - 1):
+                own, other = two_products(y[:], layer)
+                y = work.tile([P, N], F32, name="turned")
+                nc.vector.tensor_tensor(y[:], own[:], other[:], ADD)
+
+            own, other = two_products(y[:], LAYERS - 1)
+            nc.vector.tensor_tensor(windows[r][:].indirect(offsets[:]), own[:], other[:], ADD)
+            nc.sync.dma_start(out[r * P : (r + 1) * P, :], windows[r][:])

@@ -1,6 +1,7 @@
 import math
 
 import concourse.mybir as mybir
+from concourse.masks import make_block_diagonal, make_identity
 
 F32 = mybir.dt.float32
 U16 = mybir.dt.uint16
@@ -11,10 +12,12 @@ ABS = mybir.ActivationFunctionType.Abs
 
 P = 128
 ROWS, WIDE, N = 512, 2048, 512
-PAIRS = N // 2
 STRIDES = (1, 2, 1)
 LAYERS = len(STRIDES)
-FLOPS = LAYERS * ROWS * PAIRS * 6
+GROUP = 4
+CHUNKS = N // P
+SMALL = CHUNKS * GROUP
+FLOPS = LAYERS * ROWS * (N // 2) * 6
 
 
 def tile_butterflymodule_kernel(tc, base, data, angles, offs, out):
@@ -23,33 +26,47 @@ def tile_butterflymodule_kernel(tc, base, data, angles, offs, out):
         tc.tile_pool(name="held", bufs=1) as held,
         tc.tile_pool(name="rows", bufs=ROWS // P) as rows,
         tc.tile_pool(name="work", bufs=2) as work,
+        tc.psum_pool(name="flip", bufs=2) as flip,
+        tc.psum_pool(name="banks", bufs=4) as banks,
     ):
         offsets = held.tile([P, N // 16], U16, name="offsets")
         nc.sync.dma_start(offsets[:], offs)
 
-        angle = held.tile([P, LAYERS, PAIRS], F32, name="angle")
-        nc.sync.dma_start(
-            angle[:].rearrange("k l q -> k (l q)"),
-            angles.rearrange("l q -> (l q)").partition_broadcast(P),
-        )
+        angle = held.tile([P, LAYERS, SMALL // 2], F32, name="angle")
+        by_group = angles.rearrange("l (c g x) -> g (l c) x", c=CHUNKS, x=2)
+        for m in range(GROUP):
+            nc.sync.dma_start(angle[m:P:GROUP].rearrange("g l (c x) -> g (l c) x", x=2), by_group)
 
-        windows, fresh = [], []
+        fresh, windows = [], []
         for r in range(ROWS // P):
             fresh.append(rows.tile([P, N], F32, name="fresh"))
             nc.sync.dma_start(fresh[r][:], data[r * P : (r + 1) * P, :])
+        for r in range(ROWS // P):
             windows.append(rows.tile([P, WIDE], F32, name="window"))
             nc.sync.dma_start(windows[r][:], base[r * P : (r + 1) * P, :])
 
-        size = held.tile([P, LAYERS, PAIRS], F32, name="size")
-        cos = held.tile([P, LAYERS, PAIRS], F32, name="cos")
-        sin = held.tile([P, LAYERS, PAIRS], F32, name="sin")
-        minus_sin = held.tile([P, LAYERS, PAIRS], F32, name="minus_sin")
+        identity = held.tile([P, P], F32, name="identity")
+        make_identity(nc, identity[:])
+        same_group = held.tile([P, P], F32, name="same_group")
+        make_block_diagonal(nc, same_group[:], GROUP)
+
+        unit = held.tile([P, SMALL], F32, name="unit")
+        nc.vector.reduce_sum(
+            unit[:].rearrange("k (c d) -> k c d", d=GROUP),
+            identity[:].rearrange("k (g d) -> k d g", d=GROUP).unsqueeze(1).broadcast_to([P, CHUNKS, GROUP, P // GROUP]),
+            axis=mybir.AxisListType.X,
+        )
+
+        size = held.tile([P, LAYERS, SMALL // 2], F32, name="size")
+        cos = held.tile([P, LAYERS, SMALL // 2], F32, name="cos")
+        sin = held.tile([P, LAYERS, SMALL // 2], F32, name="sin")
+        minus_sin = held.tile([P, LAYERS, SMALL // 2], F32, name="minus_sin")
         nc.scalar.activation(size[:], angle[:], ABS)
         nc.scalar.activation(cos[:], size[:], SIN, bias=math.pi / 2, scale=-1.0)
         nc.scalar.activation(sin[:], angle[:], SIN)
         nc.scalar.activation(minus_sin[:], angle[:], SIN, scale=-1.0)
 
-        def two_products(y, layer):
+        def two_products(own, other, y, layer):
             s = STRIDES[layer]
 
             def members(columns):
@@ -58,21 +75,50 @@ def tile_butterflymodule_kernel(tc, base, data, angles, offs, out):
             def per_pair(values):
                 return values[:, layer].rearrange("k (g s) -> k g s", s=s)
 
-            own = work.tile([P, N], F32, name="own")
-            other = work.tile([P, N], F32, name="other")
-            for_both = per_pair(cos).unsqueeze(2).broadcast_to([P, PAIRS // s, 2, s])
-            nc.vector.tensor_tensor(members(own[:]), members(y), for_both, MULT)
-            nc.vector.tensor_tensor(members(other[:])[:, :, 0], members(y)[:, :, 1], per_pair(minus_sin), MULT)
-            nc.vector.tensor_tensor(members(other[:])[:, :, 1], members(y)[:, :, 0], per_pair(sin), MULT)
-            return own, other
+            for_both = per_pair(cos).unsqueeze(2).broadcast_to([P, SMALL // 2 // s, 2, s])
+            nc.vector.tensor_tensor(members(own), members(y), for_both, MULT)
+            nc.vector.tensor_tensor(members(other)[:, :, 0], members(y)[:, :, 1], per_pair(minus_sin), MULT)
+            nc.vector.tensor_tensor(members(other)[:, :, 1], members(y)[:, :, 0], per_pair(sin), MULT)
+
+        y = unit
+        for layer in range(LAYERS - 1):
+            own = work.tile([P, SMALL], F32, name="own")
+            other = work.tile([P, SMALL], F32, name="other")
+            two_products(own[:], other[:], y[:], layer)
+            y = work.tile([P, SMALL], F32, name="turned")
+            nc.vector.tensor_tensor(y[:], own[:], other[:], ADD)
+        entries = held.tile([P, 2, SMALL], F32, name="entries")
+        two_products(entries[:, 0], entries[:, 1], y[:], LAYERS - 1)
+
+        matrix = held.tile([P, CHUNKS, 2, P], F32, name="matrix")
+        spread = [P, 2, P // GROUP, GROUP]
+        for c in range(CHUNKS):
+            nc.vector.tensor_tensor(
+                matrix[:, c].rearrange("k t (g d) -> k t g d", d=GROUP),
+                entries[:, :, c * GROUP : (c + 1) * GROUP].unsqueeze(2).broadcast_to(spread),
+                same_group[:].rearrange("k (g d) -> k g d", d=GROUP).unsqueeze(1).broadcast_to(spread),
+                MULT,
+            )
+
+        flipped = []
+        for r in range(ROWS // P):
+            flipped_bank = flip.tile([P, N], F32, name="flipped_bank")
+            for c in range(CHUNKS):
+                nc.tensor.transpose(flipped_bank[:, c * P : (c + 1) * P], fresh[r][:, c * P : (c + 1) * P], identity[:])
+            flipped.append(rows.tile([P, N], F32, name="flipped"))
+            nc.scalar.copy(flipped[r][:], flipped_bank[:])
 
         for r in range(ROWS // P):
-            y = fresh[r]
-            for layer in range(LAYERS - 1):
-                own, other = two_products(y[:], layer)
-                y = work.tile([P, N], F32, name="turned")
-                nc.vector.tensor_tensor(y[:], own[:], other[:], ADD)
+            products = rows.tile([P, 2, N], F32, name="products")
+            for h in range(CHUNKS // 2):
+                bank = banks.tile([P, 2, 2, P], F32, name="bank")
+                for i in range(2):
+                    c = 2 * h + i
+                    nc.tensor.matmul(bank[:, i], lhsT=flipped[r][:, c * P : (c + 1) * P], rhs=matrix[:, c], start=True, stop=True)
+                nc.scalar.copy(
+                    products[:, :, 2 * h * P : (2 * h + 2) * P].rearrange("k t (i j) -> k i t j", i=2),
+                    bank[:],
+                )
 
-            own, other = two_products(y[:], LAYERS - 1)
-            nc.vector.tensor_tensor(windows[r][:].indirect(offsets[:]), own[:], other[:], ADD)
+            nc.vector.tensor_tensor(windows[r][:].indirect(offsets[:]), products[:, 0], products[:, 1], ADD)
             nc.sync.dma_start(out[r * P : (r + 1) * P, :], windows[r][:])

@@ -26,16 +26,18 @@ def tile_butterflymodule_kernel(tc, base, data, angles, offs, out):
         tc.tile_pool(name="held", bufs=1) as held,
         tc.tile_pool(name="rows", bufs=ROWS // P) as rows,
         tc.tile_pool(name="work", bufs=2) as work,
+        tc.psum_pool(name="once", bufs=1) as once,
         tc.psum_pool(name="flip", bufs=2) as flip,
         tc.psum_pool(name="banks", bufs=4) as banks,
     ):
         offsets = held.tile([P, N // 16], U16, name="offsets")
         nc.sync.dma_start(offsets[:], offs)
 
-        angle = held.tile([P, LAYERS, SMALL // 2], F32, name="angle")
-        by_group = angles.rearrange("l (c g x) -> g (l c) x", c=CHUNKS, x=2)
-        for m in range(GROUP):
-            nc.sync.dma_start(angle[m:P:GROUP].rearrange("g l (c x) -> g (l c) x", x=2), by_group)
+        group_angle = held.tile([P // GROUP, LAYERS, SMALL // 2], F32, name="group_angle")
+        nc.sync.dma_start(
+            group_angle[:].rearrange("g l (c x) -> g (l c) x", x=2),
+            angles.rearrange("l (c g x) -> g (l c) x", c=CHUNKS, x=2),
+        )
 
         fresh, windows = [], []
         for r in range(ROWS // P):
@@ -44,6 +46,19 @@ def tile_butterflymodule_kernel(tc, base, data, angles, offs, out):
         for r in range(ROWS // P):
             windows.append(rows.tile([P, WIDE], F32, name="window"))
             nc.sync.dma_start(windows[r][:], base[r * P : (r + 1) * P, :])
+
+        serves = held.tile([P // GROUP, P], F32, name="serves")
+        nc.gpsimd.memset(serves[:], 1.0)
+        nc.gpsimd.affine_select(
+            out=serves[:], in_=serves[:], compare_op=mybir.AluOpType.is_ge, fill=0.0,
+            base=0, pattern=[[1, P]], channel_multiplier=-GROUP,
+        )
+        nc.gpsimd.affine_select(
+            out=serves[:], in_=serves[:], compare_op=mybir.AluOpType.is_ge, fill=0.0,
+            base=GROUP - 1, pattern=[[-1, P]], channel_multiplier=GROUP,
+        )
+        angle = once.tile([P, LAYERS, SMALL // 2], F32, name="angle")
+        nc.tensor.matmul(angle[:], lhsT=serves[:], rhs=group_angle[:], start=True, stop=True)
 
         identity = held.tile([P, P], F32, name="identity")
         make_identity(nc, identity[:])

@@ -26,18 +26,21 @@ def tile_butterflymodule_kernel(tc, base, data, angles, offs, out):
         tc.tile_pool(name="held", bufs=1) as held,
         tc.tile_pool(name="rows", bufs=ROWS // P) as rows,
         tc.tile_pool(name="work", bufs=2) as work,
-        tc.psum_pool(name="once", bufs=1) as once,
-        tc.psum_pool(name="flip", bufs=2) as flip,
+        tc.psum_pool(name="flip", bufs=ROWS // P) as flip,
         tc.psum_pool(name="banks", bufs=4) as banks,
     ):
+        angle = held.tile([P, LAYERS, SMALL // 2], F32, name="angle")
+        by_group = angles.rearrange("l (c g x) -> g (l c) x", c=CHUNKS, x=2)
+        for m in range(GROUP):
+            queue = nc.sync if m % 2 == 0 else nc.scalar
+            queue.dma_start(angle[m:P:GROUP].rearrange("g l (c x) -> g (l c) x", x=2), by_group)
+
+        early = held.tile([P, 1], F32, name="early")
+        nc.vector.memset(early[:], 0.0)
+        nc.scalar.activation(early[:], early[:], SIN)
+
         offsets = held.tile([P, N // 16], U16, name="offsets")
         nc.sync.dma_start(offsets[:], offs)
-
-        group_angle = held.tile([P // GROUP, LAYERS, SMALL // 2], F32, name="group_angle")
-        nc.sync.dma_start(
-            group_angle[:].rearrange("g l (c x) -> g (l c) x", x=2),
-            angles.rearrange("l (c g x) -> g (l c) x", c=CHUNKS, x=2),
-        )
 
         fresh, windows = [], []
         for r in range(ROWS // P):
@@ -46,19 +49,6 @@ def tile_butterflymodule_kernel(tc, base, data, angles, offs, out):
         for r in range(ROWS // P):
             windows.append(rows.tile([P, WIDE], F32, name="window"))
             nc.sync.dma_start(windows[r][:], base[r * P : (r + 1) * P, :])
-
-        serves = held.tile([P // GROUP, P], F32, name="serves")
-        nc.gpsimd.memset(serves[:], 1.0)
-        nc.gpsimd.affine_select(
-            out=serves[:], in_=serves[:], compare_op=mybir.AluOpType.is_ge, fill=0.0,
-            base=0, pattern=[[1, P]], channel_multiplier=-GROUP,
-        )
-        nc.gpsimd.affine_select(
-            out=serves[:], in_=serves[:], compare_op=mybir.AluOpType.is_ge, fill=0.0,
-            base=GROUP - 1, pattern=[[-1, P]], channel_multiplier=GROUP,
-        )
-        angle = once.tile([P, LAYERS, SMALL // 2], F32, name="angle")
-        nc.tensor.matmul(angle[:], lhsT=serves[:], rhs=group_angle[:], start=True, stop=True)
 
         identity = held.tile([P, P], F32, name="identity")
         make_identity(nc, identity[:])
@@ -74,12 +64,11 @@ def tile_butterflymodule_kernel(tc, base, data, angles, offs, out):
 
         size = held.tile([P, LAYERS, SMALL // 2], F32, name="size")
         cos = held.tile([P, LAYERS, SMALL // 2], F32, name="cos")
-        sin = held.tile([P, LAYERS, SMALL // 2], F32, name="sin")
-        minus_sin = held.tile([P, LAYERS, SMALL // 2], F32, name="minus_sin")
+        signed_sin = held.tile([P, LAYERS, 2, SMALL // 2], F32, name="signed_sin")
+        nc.scalar.activation(signed_sin[:, :, 1], angle[:], SIN)
+        nc.vector.tensor_scalar_mul(signed_sin[:, :, 0], signed_sin[:, :, 1], -1.0)
         nc.scalar.activation(size[:], angle[:], ABS)
         nc.scalar.activation(cos[:], size[:], SIN, bias=math.pi / 2, scale=-1.0)
-        nc.scalar.activation(sin[:], angle[:], SIN)
-        nc.scalar.activation(minus_sin[:], angle[:], SIN, scale=-1.0)
 
         def two_products(own, other, y, layer):
             s = STRIDES[layer]
@@ -87,13 +76,10 @@ def tile_butterflymodule_kernel(tc, base, data, angles, offs, out):
             def members(columns):
                 return columns.rearrange("k (g e s) -> k g e s", e=2, s=s)
 
-            def per_pair(values):
-                return values[:, layer].rearrange("k (g s) -> k g s", s=s)
-
-            for_both = per_pair(cos).unsqueeze(2).broadcast_to([P, SMALL // 2 // s, 2, s])
+            for_both = cos[:, layer].rearrange("k (g s) -> k g s", s=s).unsqueeze(2).broadcast_to([P, SMALL // 2 // s, 2, s])
+            by_member = signed_sin[:, layer].rearrange("k e (g s) -> k g e s", s=s)
             nc.vector.tensor_tensor(members(own), members(y), for_both, MULT)
-            nc.vector.tensor_tensor(members(other)[:, :, 0], members(y)[:, :, 1], per_pair(minus_sin), MULT)
-            nc.vector.tensor_tensor(members(other)[:, :, 1], members(y)[:, :, 0], per_pair(sin), MULT)
+            nc.vector.tensor_tensor(members(other), members(y)[:, :, ::-1], by_member, MULT)
 
         y = unit
         for layer in range(LAYERS - 1):

@@ -29,11 +29,12 @@ def tile_butterflymodule_kernel(tc, base, data, angles, offs, out):
         tc.psum_pool(name="flip", bufs=ROWS // P) as flip,
         tc.psum_pool(name="banks", bufs=4) as banks,
     ):
-        angle = held.tile([P, LAYERS, SMALL // 2], F32, name="angle")
-        by_group = angles.rearrange("l (c g x) -> g (l c) x", c=CHUNKS, x=2)
+        padded = held.tile([P, LAYERS, CHUNKS, 8], F32, name="padded")
+        by_group = angles.rearrange("l (c g x) -> g l c x", c=CHUNKS, x=2)
         for m in range(GROUP):
             queue = nc.sync if m % 2 == 0 else nc.scalar
-            queue.dma_start(angle[m:P:GROUP].rearrange("g l (c x) -> g (l c) x", x=2), by_group)
+            queue.dma_start(padded[m:P:GROUP, :, :, 0:2], by_group)
+        angle = padded[:, :, :, 0:2]
 
         early = held.tile([P, 1], F32, name="early")
         nc.vector.memset(early[:], 0.0)
@@ -65,9 +66,9 @@ def tile_butterflymodule_kernel(tc, base, data, angles, offs, out):
         size = held.tile([P, LAYERS, SMALL // 2], F32, name="size")
         cos = held.tile([P, LAYERS, SMALL // 2], F32, name="cos")
         signed_sin = held.tile([P, LAYERS, 2, SMALL // 2], F32, name="signed_sin")
-        nc.scalar.activation(signed_sin[:, :, 1], angle[:], SIN)
+        nc.scalar.activation(signed_sin[:, :, 1].rearrange("k l (c x) -> k l c x", x=2), angle, SIN)
         nc.vector.tensor_scalar_mul(signed_sin[:, :, 0], signed_sin[:, :, 1], -1.0)
-        nc.scalar.activation(size[:], angle[:], ABS)
+        nc.scalar.activation(size[:].rearrange("k l (c x) -> k l c x", x=2), angle, ABS)
         nc.scalar.activation(cos[:], size[:], SIN, bias=math.pi / 2, scale=-1.0)
 
         def two_products(own, other, y, layer):

@@ -7,8 +7,8 @@ F32 = mybir.dt.float32
 U16 = mybir.dt.uint16
 MULT = mybir.AluOpType.mult
 ADD = mybir.AluOpType.add
+MIN = mybir.AluOpType.min
 SIN = mybir.ActivationFunctionType.Sin
-ABS = mybir.ActivationFunctionType.Abs
 
 P = 128
 ROWS, WIDE, N = 512, 2048, 512
@@ -16,7 +16,6 @@ STRIDES = (1, 2, 1)
 LAYERS = len(STRIDES)
 GROUP = 4
 CHUNKS = N // P
-SMALL = CHUNKS * GROUP
 FLOPS = LAYERS * ROWS * (N // 2) * 6
 
 
@@ -25,7 +24,6 @@ def tile_butterflymodule_kernel(tc, base, data, angles, offs, out):
     with (
         tc.tile_pool(name="held", bufs=1) as held,
         tc.tile_pool(name="rows", bufs=ROWS // P) as rows,
-        tc.tile_pool(name="work", bufs=2) as work,
         tc.psum_pool(name="flip", bufs=ROWS // P) as flip,
         tc.psum_pool(name="banks", bufs=4) as banks,
     ):
@@ -53,52 +51,60 @@ def tile_butterflymodule_kernel(tc, base, data, angles, offs, out):
 
         identity = held.tile([P, P], F32, name="identity")
         make_identity(nc, identity[:])
-        same_group = held.tile([P, P], F32, name="same_group")
-        make_block_diagonal(nc, same_group[:], GROUP)
+        signed_group = held.tile([P, 2, P], F32, name="signed_group")
+        make_block_diagonal(nc, signed_group[:, 0], GROUP)
+        plain_pairs = signed_group[:, 0].rearrange("k (j e) -> k j e", e=2)
+        signed_pairs = signed_group[:, 1].rearrange("k (j e) -> k j e", e=2)
+        nc.gpsimd.tensor_scalar_mul(signed_pairs[:, :, 0], plain_pairs[:, :, 0], -1.0)
+        nc.gpsimd.tensor_scalar_mul(signed_pairs[:, :, 1], plain_pairs[:, :, 1], 1.0)
 
-        unit = held.tile([P, SMALL], F32, name="unit")
-        nc.vector.reduce_sum(
-            unit[:].rearrange("k (c d) -> k c d", d=GROUP),
-            identity[:].rearrange("k (g d) -> k d g", d=GROUP).unsqueeze(1).broadcast_to([P, CHUNKS, GROUP, P // GROUP]),
-            axis=mybir.AxisListType.X,
+        place = held.tile([P, GROUP], F32, name="place")
+        nc.vector.reduce_sum(place[:], identity[:].rearrange("k (g d) -> k d g", d=GROUP), axis=mybir.AxisListType.X)
+        high = held.tile([P, 2], F32, name="high")
+        nc.vector.reduce_sum(high[:], place[:].rearrange("k (h e) -> k h e", e=2), axis=mybir.AxisListType.X)
+        pick = held.tile([P, 2, GROUP, 4], F32, name="pick")
+        nc.vector.memset(pick[:], 0.0)
+        first = pick[:, 0].rearrange("k (a b) (f x) -> k a b f x", b=2, x=2)
+        by_low = place[:].rearrange("k (x b) -> k b x", b=2)
+        both = [P, 2, 2]
+        nc.vector.tensor_copy(first[:, :, :, 0, :], by_low.unsqueeze(1).broadcast_to([P, 2, 2, 2]))
+        nc.vector.tensor_scalar_mul(first[:, :, 0, 1, :], by_low[:, 1].unsqueeze(1).broadcast_to(both), -1.0)
+        nc.vector.tensor_copy(first[:, :, 1, 1, :], by_low[:, 0].unsqueeze(1).broadcast_to(both))
+        second = pick[:, 1].rearrange("k (a b) t -> k a (b t)", b=2)
+        nc.vector.tensor_copy(second[:, :, 0:6:5], high[:].unsqueeze(2).broadcast_to(both))
+        nc.vector.tensor_scalar_mul(second[:, 0, 2:8:5], high[:, 1:2].broadcast_to([P, 2]), -1.0)
+        nc.vector.tensor_copy(second[:, 1, 2:8:5], high[:, 0:1].broadcast_to([P, 2]))
+
+        trig = held.tile([P, LAYERS, CHUNKS, 2, 2], F32, name="trig")
+        minus_size = held.tile([P, LAYERS, CHUNKS, 2], F32, name="minus_size")
+        nc.scalar.activation(trig[:, :, :, 1, :], angle, SIN)
+        nc.vector.scalar_tensor_tensor(minus_size[:], angle, -1.0, angle, MULT, MIN)
+        nc.scalar.activation(trig[:, :, :, 0, :], minus_size[:], SIN, bias=math.pi / 2)
+
+        terms = held.tile([P, 2, CHUNKS, GROUP, 4], F32, name="terms")
+        nc.vector.tensor_tensor(
+            terms[:],
+            trig[:, 0:2].rearrange("k l c f x -> k l c (f x)").unsqueeze(3).broadcast_to([P, 2, CHUNKS, GROUP, 4]),
+            pick[:].unsqueeze(2).broadcast_to([P, 2, CHUNKS, GROUP, 4]),
+            MULT,
         )
+        factor = held.tile([P, 2, CHUNKS, GROUP], F32, name="factor")
+        nc.vector.reduce_sum(factor[:], terms[:], axis=mybir.AxisListType.X)
+        turned = held.tile([P, CHUNKS, 2, 2], F32, name="turned")
+        nc.vector.tensor_tensor(turned[:].rearrange("k c a b -> k c (a b)"), factor[:, 0], factor[:, 1], MULT)
 
-        size = held.tile([P, LAYERS, SMALL // 2], F32, name="size")
-        cos = held.tile([P, LAYERS, SMALL // 2], F32, name="cos")
-        signed_sin = held.tile([P, LAYERS, 2, SMALL // 2], F32, name="signed_sin")
-        nc.scalar.activation(signed_sin[:, :, 1].rearrange("k l (c x) -> k l c x", x=2), angle, SIN)
-        nc.vector.tensor_scalar_mul(signed_sin[:, :, 0], signed_sin[:, :, 1], -1.0)
-        nc.scalar.activation(size[:].rearrange("k l (c x) -> k l c x", x=2), angle, ABS)
-        nc.scalar.activation(cos[:], size[:], SIN, bias=math.pi / 2, scale=-1.0)
-
-        def two_products(own, other, y, layer):
-            s = STRIDES[layer]
-
-            def members(columns):
-                return columns.rearrange("k (g e s) -> k g e s", e=2, s=s)
-
-            for_both = cos[:, layer].rearrange("k (g s) -> k g s", s=s).unsqueeze(2).broadcast_to([P, SMALL // 2 // s, 2, s])
-            by_member = signed_sin[:, layer].rearrange("k e (g s) -> k g e s", s=s)
-            nc.vector.tensor_tensor(members(own), members(y), for_both, MULT)
-            nc.vector.tensor_tensor(members(other), members(y)[:, :, ::-1], by_member, MULT)
-
-        y = unit
-        for layer in range(LAYERS - 1):
-            own = work.tile([P, SMALL], F32, name="own")
-            other = work.tile([P, SMALL], F32, name="other")
-            two_products(own[:], other[:], y[:], layer)
-            y = work.tile([P, SMALL], F32, name="turned")
-            nc.vector.tensor_tensor(y[:], own[:], other[:], ADD)
-        entries = held.tile([P, 2, SMALL], F32, name="entries")
-        two_products(entries[:, 0], entries[:, 1], y[:], LAYERS - 1)
+        entries = held.tile([P, 2, CHUNKS, 2, 2], F32, name="entries")
+        for_both = [P, CHUNKS, 2, 2]
+        nc.vector.tensor_tensor(entries[:, 0], turned[:], trig[:, 2, :, 0, :].unsqueeze(3).broadcast_to(for_both), MULT)
+        nc.vector.tensor_tensor(entries[:, 1], turned[:, :, :, ::-1], trig[:, 2, :, 1, :].unsqueeze(3).broadcast_to(for_both), MULT)
 
         matrix = held.tile([P, CHUNKS, 2, P], F32, name="matrix")
         spread = [P, 2, P // GROUP, GROUP]
         for c in range(CHUNKS):
             nc.vector.tensor_tensor(
                 matrix[:, c].rearrange("k t (g d) -> k t g d", d=GROUP),
-                entries[:, :, c * GROUP : (c + 1) * GROUP].unsqueeze(2).broadcast_to(spread),
-                same_group[:].rearrange("k (g d) -> k g d", d=GROUP).unsqueeze(1).broadcast_to(spread),
+                entries[:, :, c].rearrange("k t a b -> k t (a b)").unsqueeze(2).broadcast_to(spread),
+                signed_group[:].rearrange("k t (g d) -> k t g d", d=GROUP),
                 MULT,
             )
 
@@ -112,15 +118,13 @@ def tile_butterflymodule_kernel(tc, base, data, angles, offs, out):
 
         for r in range(ROWS // P):
             products = rows.tile([P, 2, N], F32, name="products")
-            for h in range(CHUNKS // 2):
-                bank = banks.tile([P, 2, 2, P], F32, name="bank")
-                for i in range(2):
-                    c = 2 * h + i
-                    nc.tensor.matmul(bank[:, i], lhsT=flipped[r][:, c * P : (c + 1) * P], rhs=matrix[:, c], start=True, stop=True)
-                nc.scalar.copy(
-                    products[:, :, 2 * h * P : (2 * h + 2) * P].rearrange("k t (i j) -> k i t j", i=2),
-                    bank[:],
-                )
+            for c in range(CHUNKS):
+                bank = banks.tile([P, 2, P], F32, name="bank")
+                nc.tensor.matmul(bank[:], lhsT=flipped[r][:, c * P : (c + 1) * P], rhs=matrix[:, c], start=True, stop=True)
+                if r == 0 and c % 2 == 1:
+                    nc.vector.tensor_copy(products[:, :, c * P : (c + 1) * P], bank[:])
+                else:
+                    nc.scalar.copy(products[:, :, c * P : (c + 1) * P], bank[:])
 
             nc.vector.tensor_tensor(windows[r][:].indirect(offsets[:]), products[:, 0], products[:, 1], ADD)
             nc.sync.dma_start(out[r * P : (r + 1) * P, :], windows[r][:])

@@ -15,6 +15,8 @@ ROWS, WIDE, N = 512, 2048, 512
 STRIDES = (1, 2, 1)
 LAYERS = len(STRIDES)
 GROUP = 4
+BLOCKS = ROWS // P
+AHEAD = 2
 CHUNKS = N // P
 FLOPS = LAYERS * ROWS * (N // 2) * 6
 
@@ -23,8 +25,8 @@ def tile_butterflymodule_kernel(tc, base, data, angles, offs, out):
     nc = tc.nc
     with (
         tc.tile_pool(name="held", bufs=1) as held,
-        tc.tile_pool(name="rows", bufs=ROWS // P) as rows,
-        tc.psum_pool(name="flip", bufs=ROWS // P) as flip,
+        tc.tile_pool(name="rows", bufs=BLOCKS) as rows,
+        tc.psum_pool(name="flip_banks", bufs=BLOCKS) as flip_banks,
         tc.psum_pool(name="banks", bufs=4) as banks,
     ):
         padded = held.tile([P, LAYERS, CHUNKS, 8], F32, name="padded")
@@ -42,10 +44,10 @@ def tile_butterflymodule_kernel(tc, base, data, angles, offs, out):
         nc.sync.dma_start(offsets[:], offs)
 
         fresh, windows = [], []
-        for r in range(ROWS // P):
+        for r in range(BLOCKS):
             fresh.append(rows.tile([P, N], F32, name="fresh"))
             nc.sync.dma_start(fresh[r][:], data[r * P : (r + 1) * P, :])
-        for r in range(ROWS // P):
+        for r in range(BLOCKS):
             windows.append(rows.tile([P, WIDE], F32, name="window"))
             nc.sync.dma_start(windows[r][:], base[r * P : (r + 1) * P, :])
 
@@ -109,14 +111,21 @@ def tile_butterflymodule_kernel(tc, base, data, angles, offs, out):
             )
 
         flipped = []
-        for r in range(ROWS // P):
-            flipped_bank = flip.tile([P, N], F32, name="flipped_bank")
+
+        def flip(r):
+            flipped_bank = flip_banks.tile([P, N], F32, name="flipped_bank")
             for c in range(CHUNKS):
-                nc.tensor.transpose(flipped_bank[:, c * P : (c + 1) * P], fresh[r][:, c * P : (c + 1) * P], identity[:])
+                block = fresh[r][:, c * P : (c + 1) * P]
+                if r == 0:
+                    nc.tensor.matmul(flipped_bank[:, c * P : (c + 1) * P], lhsT=block, rhs=identity[:], start=True, stop=True)
+                else:
+                    nc.tensor.transpose(flipped_bank[:, c * P : (c + 1) * P], block, identity[:])
             flipped.append(rows.tile([P, N], F32, name="flipped"))
             nc.scalar.copy(flipped[r][:], flipped_bank[:])
 
-        for r in range(ROWS // P):
+        for r in range(AHEAD):
+            flip(r)
+        for r in range(BLOCKS):
             products = rows.tile([P, 2, N], F32, name="products")
             for c in range(CHUNKS):
                 bank = banks.tile([P, 2, P], F32, name="bank")
@@ -125,6 +134,8 @@ def tile_butterflymodule_kernel(tc, base, data, angles, offs, out):
                     nc.vector.tensor_copy(products[:, :, c * P : (c + 1) * P], bank[:])
                 else:
                     nc.scalar.copy(products[:, :, c * P : (c + 1) * P], bank[:])
+            if r + AHEAD < BLOCKS:
+                flip(r + AHEAD)
 
             nc.vector.tensor_tensor(windows[r][:].indirect(offsets[:]), products[:, 0], products[:, 1], ADD)
             nc.sync.dma_start(out[r * P : (r + 1) * P, :], windows[r][:])

@@ -26,8 +26,7 @@ def tile_butterflymodule_kernel(tc, base, data, angles, offs, out):
     with (
         tc.tile_pool(name="held", bufs=1) as held,
         tc.tile_pool(name="rows", bufs=BLOCKS) as rows,
-        tc.psum_pool(name="flip_banks", bufs=BLOCKS) as flip_banks,
-        tc.psum_pool(name="banks", bufs=4) as banks,
+        tc.psum_pool(name="banks", bufs=8) as banks,
     ):
         padded = held.tile([P, LAYERS, CHUNKS, 8], F32, name="padded")
         by_group = angles.rearrange("l (c g x) -> g l c x", c=CHUNKS, x=2)
@@ -113,7 +112,7 @@ def tile_butterflymodule_kernel(tc, base, data, angles, offs, out):
         flipped = []
 
         def flip(r):
-            flipped_bank = flip_banks.tile([P, N], F32, name="flipped_bank")
+            flipped_bank = banks.tile([P, N], F32, name="flipped_bank", tag="bank")
             for c in range(CHUNKS):
                 block = fresh[r][:, c * P : (c + 1) * P]
                 if r == 0:
@@ -128,7 +127,7 @@ def tile_butterflymodule_kernel(tc, base, data, angles, offs, out):
         for r in range(BLOCKS):
             products = rows.tile([P, 2, N], F32, name="products")
             for c in range(CHUNKS):
-                bank = banks.tile([P, 2, P], F32, name="bank")
+                bank = banks.tile([P, 2, P], F32, name="bank", tag="bank")
                 nc.tensor.matmul(bank[:], lhsT=flipped[r][:, c * P : (c + 1) * P], rhs=matrix[:, c], start=True, stop=True)
                 if r == 0 and c % 2 == 1:
                     nc.vector.tensor_copy(products[:, :, c * P : (c + 1) * P], bank[:])

@@ -115,7 +115,7 @@ def tile_butterflymodule_kernel(tc, base, data, angles, offs, out):
             flipped_bank = banks.tile([P, N], F32, name="flipped_bank", tag="bank")
             for c in range(CHUNKS):
                 block = fresh[r][:, c * P : (c + 1) * P]
-                if r == 0:
+                if r == AHEAD - 1:
                     nc.tensor.matmul(flipped_bank[:, c * P : (c + 1) * P], lhsT=block, rhs=identity[:], start=True, stop=True)
                 else:
                     nc.tensor.transpose(flipped_bank[:, c * P : (c + 1) * P], block, identity[:])

@@ -127,12 +127,16 @@ def tile_butterflymodule_kernel(tc, base, data, angles, offs, out):
         for r in range(BLOCKS):
             products = rows.tile([P, 2, N], F32, name="products")
             for c in range(CHUNKS):
-                bank = banks.tile([P, 2, P], F32, name="bank", tag="bank")
-                nc.tensor.matmul(bank[:], lhsT=flipped[r][:, c * P : (c + 1) * P], rhs=matrix[:, c], start=True, stop=True)
-                if r == 0 and c % 2 == 1:
-                    nc.vector.tensor_copy(products[:, :, c * P : (c + 1) * P], bank[:])
+                here = slice(c * P, (c + 1) * P)
+                if r == 0:
+                    for t, copy_out in enumerate((nc.scalar.copy, nc.vector.tensor_copy)):
+                        half_bank = banks.tile([P, P], F32, name="half_bank", tag="bank")
+                        nc.tensor.matmul(half_bank[:], lhsT=flipped[r][:, here], rhs=matrix[:, c, t], start=True, stop=True)
+                        copy_out(products[:, t, here], half_bank[:])
                 else:
-                    nc.scalar.copy(products[:, :, c * P : (c + 1) * P], bank[:])
+                    bank = banks.tile([P, 2, P], F32, name="bank", tag="bank")
+                    nc.tensor.matmul(bank[:], lhsT=flipped[r][:, here], rhs=matrix[:, c], start=True, stop=True)
+                    nc.scalar.copy(products[:, :, here], bank[:])
             if r + AHEAD < BLOCKS:
                 flip(r + AHEAD)
 

@@ -9,6 +9,7 @@ MULT = mybir.AluOpType.mult
 ADD = mybir.AluOpType.add
 MIN = mybir.AluOpType.min
 SIN = mybir.ActivationFunctionType.Sin
+COS, SINE = 0, 1
 
 P = 128
 ROWS, WIDE, N = 512, 2048, 512
@@ -26,6 +27,7 @@ def tile_butterflymodule_kernel(tc, base, data, angles, offs, out):
     with (
         tc.tile_pool(name="held", bufs=1) as held,
         tc.tile_pool(name="rows", bufs=BLOCKS) as rows,
+        tc.tile_pool(name="in_turn", bufs=BLOCKS + 2) as in_turn,
         tc.psum_pool(name="banks", bufs=8) as banks,
     ):
         padded = held.tile([P, LAYERS, CHUNKS, 8], F32, name="padded")
@@ -63,41 +65,49 @@ def tile_butterflymodule_kernel(tc, base, data, angles, offs, out):
         nc.vector.reduce_sum(place[:], identity[:].rearrange("k (g d) -> k d g", d=GROUP), axis=mybir.AxisListType.X)
         high = held.tile([P, 2], F32, name="high")
         nc.vector.reduce_sum(high[:], place[:].rearrange("k (h e) -> k h e", e=2), axis=mybir.AxisListType.X)
-        pick = held.tile([P, 2, GROUP, 4], F32, name="pick")
+        pick = held.tile([P, 2, 2, GROUP, 2], F32, name="pick")
         nc.vector.memset(pick[:], 0.0)
-        first = pick[:, 0].rearrange("k (a b) (f x) -> k a b f x", b=2, x=2)
         by_low = place[:].rearrange("k (x b) -> k b x", b=2)
         both = [P, 2, 2]
-        nc.vector.tensor_copy(first[:, :, :, 0, :], by_low.unsqueeze(1).broadcast_to([P, 2, 2, 2]))
-        nc.vector.tensor_scalar_mul(first[:, :, 0, 1, :], by_low[:, 1].unsqueeze(1).broadcast_to(both), -1.0)
-        nc.vector.tensor_copy(first[:, :, 1, 1, :], by_low[:, 0].unsqueeze(1).broadcast_to(both))
-        second = pick[:, 1].rearrange("k (a b) t -> k a (b t)", b=2)
-        nc.vector.tensor_copy(second[:, :, 0:6:5], high[:].unsqueeze(2).broadcast_to(both))
-        nc.vector.tensor_scalar_mul(second[:, 0, 2:8:5], high[:, 1:2].broadcast_to([P, 2]), -1.0)
-        nc.vector.tensor_copy(second[:, 1, 2:8:5], high[:, 0:1].broadcast_to([P, 2]))
+        first_cos = pick[:, COS, 0].rearrange("k (a b) x -> k a b x", b=2)
+        first_sin = pick[:, SINE, 0].rearrange("k (a b) x -> k a b x", b=2)
+        nc.vector.tensor_copy(first_cos, by_low.unsqueeze(1).broadcast_to([P, 2, 2, 2]))
+        nc.vector.tensor_scalar_mul(first_sin[:, :, 0], by_low[:, 1].unsqueeze(1).broadcast_to(both), -1.0)
+        nc.vector.tensor_copy(first_sin[:, :, 1], by_low[:, 0].unsqueeze(1).broadcast_to(both))
+        second_cos = pick[:, COS, 1].rearrange("k (a b) x -> k a (b x)", b=2)[:, :, 0:4:3]
+        second_sin = pick[:, SINE, 1].rearrange("k (a b) x -> k a (b x)", b=2)[:, :, 0:4:3]
+        nc.vector.tensor_copy(second_cos, high[:].unsqueeze(2).broadcast_to(both))
+        nc.vector.tensor_scalar_mul(second_sin[:, 0], high[:, 1:2].broadcast_to([P, 2]), -1.0)
+        nc.vector.tensor_copy(second_sin[:, 1], high[:, 0:1].broadcast_to([P, 2]))
 
-        trig = held.tile([P, LAYERS, CHUNKS, 2, 2], F32, name="trig")
+        sines = in_turn.tile([P, LAYERS, CHUNKS, 2], F32, name="sines", tag="turn")
+        cosines = in_turn.tile([P, LAYERS, CHUNKS, 2], F32, name="cosines", tag="turn")
         minus_size = held.tile([P, LAYERS, CHUNKS, 2], F32, name="minus_size")
-        nc.scalar.activation(trig[:, :, :, 1, :], angle, SIN)
+        nc.scalar.activation(sines[:], angle, SIN)
         nc.vector.scalar_tensor_tensor(minus_size[:], angle, -1.0, angle, MULT, MIN)
-        nc.scalar.activation(trig[:, :, :, 0, :], minus_size[:], SIN, bias=math.pi / 2)
+        nc.scalar.activation(cosines[:], minus_size[:], SIN, bias=math.pi / 2)
 
-        terms = held.tile([P, 2, CHUNKS, GROUP, 4], F32, name="terms")
-        nc.vector.tensor_tensor(
-            terms[:],
-            trig[:, 0:2].rearrange("k l c f x -> k l c (f x)").unsqueeze(3).broadcast_to([P, 2, CHUNKS, GROUP, 4]),
-            pick[:].unsqueeze(2).broadcast_to([P, 2, CHUNKS, GROUP, 4]),
-            MULT,
+        terms = held.tile([P, 2, 2, CHUNKS, GROUP, 2], F32, name="terms")
+        for f, function in ((SINE, sines), (COS, cosines)):
+            nc.vector.tensor_tensor(
+                terms[:, f],
+                function[:, 0:2].unsqueeze(3).broadcast_to([P, 2, CHUNKS, GROUP, 2]),
+                pick[:, f].unsqueeze(2).broadcast_to([P, 2, CHUNKS, GROUP, 2]),
+                MULT,
+            )
+        factor = held.tile([P, 2, CHUNKS * GROUP], F32, name="factor")
+        nc.vector.reduce_sum(
+            factor[:].rearrange("k l j -> k (l j)"),
+            terms[:].rearrange("k f l c j x -> k (l c j) f x"),
+            axis=mybir.AxisListType.XY,
         )
-        factor = held.tile([P, 2, CHUNKS, GROUP], F32, name="factor")
-        nc.vector.reduce_sum(factor[:], terms[:], axis=mybir.AxisListType.X)
         turned = held.tile([P, CHUNKS, 2, 2], F32, name="turned")
-        nc.vector.tensor_tensor(turned[:].rearrange("k c a b -> k c (a b)"), factor[:, 0], factor[:, 1], MULT)
+        nc.vector.tensor_tensor(turned[:].rearrange("k c a b -> k (c a b)"), factor[:, 0], factor[:, 1], MULT)
 
         entries = held.tile([P, 2, CHUNKS, 2, 2], F32, name="entries")
         for_both = [P, CHUNKS, 2, 2]
-        nc.vector.tensor_tensor(entries[:, 0], turned[:], trig[:, 2, :, 0, :].unsqueeze(3).broadcast_to(for_both), MULT)
-        nc.vector.tensor_tensor(entries[:, 1], turned[:, :, :, ::-1], trig[:, 2, :, 1, :].unsqueeze(3).broadcast_to(for_both), MULT)
+        nc.vector.tensor_tensor(entries[:, 0], turned[:], cosines[:, 2].unsqueeze(3).broadcast_to(for_both), MULT)
+        nc.vector.tensor_tensor(entries[:, 1], turned[:, :, :, ::-1], sines[:, 2].unsqueeze(3).broadcast_to(for_both), MULT)
 
         matrix = held.tile([P, CHUNKS, 2, P], F32, name="matrix")
         spread = [P, 2, P // GROUP, GROUP]
@@ -119,7 +129,7 @@ def tile_butterflymodule_kernel(tc, base, data, angles, offs, out):
                     nc.tensor.matmul(flipped_bank[:, c * P : (c + 1) * P], lhsT=block, rhs=identity[:], start=True, stop=True)
                 else:
                     nc.tensor.transpose(flipped_bank[:, c * P : (c + 1) * P], block, identity[:])
-            flipped.append(rows.tile([P, N], F32, name="flipped"))
+            flipped.append(in_turn.tile([P, N], F32, name="flipped", tag="turn"))
             nc.scalar.copy(flipped[r][:], flipped_bank[:])
 
         for r in range(AHEAD):

@@ -1,7 +1,7 @@
 import math
 
 import concourse.mybir as mybir
-from concourse.masks import make_block_diagonal, make_identity
+from concourse.masks import make_identity
 
 F32 = mybir.dt.float32
 U16 = mybir.dt.uint16
@@ -33,8 +33,7 @@ def tile_butterflymodule_kernel(tc, base, data, angles, offs, out):
         padded = held.tile([P, LAYERS, CHUNKS, 8], F32, name="padded")
         by_group = angles.rearrange("l (c g x) -> g l c x", c=CHUNKS, x=2)
         for m in range(GROUP):
-            queue = nc.sync if m % 2 == 0 else nc.scalar
-            queue.dma_start(padded[m:P:GROUP, :, :, 0:2], by_group)
+            nc.sync.dma_start(padded[m:P:GROUP, :, :, 0:2], by_group)
         angle = padded[:, :, :, 0:2]
 
         early = held.tile([P, 1], F32, name="early")
@@ -54,12 +53,18 @@ def tile_butterflymodule_kernel(tc, base, data, angles, offs, out):
 
         identity = held.tile([P, P], F32, name="identity")
         make_identity(nc, identity[:])
+        own_group = held.tile([P, P // GROUP], F32, name="own_group")
+        nc.vector.reduce_sum(own_group[:], identity[:].rearrange("k (g d) -> k g d", d=GROUP), axis=mybir.AxisListType.X)
+        signs = held.tile([P, 2, GROUP], F32, name="signs")
+        nc.vector.memset(signs[:], 1.0)
+        nc.vector.memset(signs[:, 1, 0:GROUP:2], -1.0)
         signed_group = held.tile([P, 2, P], F32, name="signed_group")
-        make_block_diagonal(nc, signed_group[:, 0], GROUP)
-        plain_pairs = signed_group[:, 0].rearrange("k (j e) -> k j e", e=2)
-        signed_pairs = signed_group[:, 1].rearrange("k (j e) -> k j e", e=2)
-        nc.gpsimd.tensor_scalar_mul(signed_pairs[:, :, 0], plain_pairs[:, :, 0], -1.0)
-        nc.gpsimd.tensor_scalar_mul(signed_pairs[:, :, 1], plain_pairs[:, :, 1], 1.0)
+        nc.vector.tensor_tensor(
+            signed_group[:].rearrange("k t (g d) -> k t g d", d=GROUP),
+            own_group[:].unsqueeze(1).unsqueeze(3).broadcast_to([P, 2, P // GROUP, GROUP]),
+            signs[:].unsqueeze(2).broadcast_to([P, 2, P // GROUP, GROUP]),
+            MULT,
+        )
 
         place = held.tile([P, GROUP], F32, name="place")
         nc.vector.reduce_sum(place[:], identity[:].rearrange("k (g d) -> k d g", d=GROUP), axis=mybir.AxisListType.X)

@@ -9,16 +9,17 @@ MULT = mybir.AluOpType.mult
 ADD = mybir.AluOpType.add
 MIN = mybir.AluOpType.min
 SIN = mybir.ActivationFunctionType.Sin
-COS, SINE = 0, 1
 
 P = 128
 ROWS, WIDE, N = 512, 2048, 512
 STRIDES = (1, 2, 1)
 LAYERS = len(STRIDES)
 GROUP = 4
+GROUPS = P // GROUP
 BLOCKS = ROWS // P
 AHEAD = 2
 CHUNKS = N // P
+WAYS = 3
 FLOPS = LAYERS * ROWS * (N // 2) * 6
 
 
@@ -30,11 +31,11 @@ def tile_butterflymodule_kernel(tc, base, data, angles, offs, out):
         tc.tile_pool(name="in_turn", bufs=BLOCKS + 2) as in_turn,
         tc.psum_pool(name="banks", bufs=8) as banks,
     ):
-        padded = held.tile([P, LAYERS, CHUNKS, 8], F32, name="padded")
-        by_group = angles.rearrange("l (c g x) -> g l c x", c=CHUNKS, x=2)
-        for m in range(GROUP):
-            nc.sync.dma_start(padded[m:P:GROUP, :, :, 0:2], by_group)
-        angle = padded[:, :, :, 0:2]
+        turns = held.tile([P, 2 * GROUPS], F32, name="turns")
+        by_row = angles.rearrange("l (c u) -> (l c) u", c=CHUNKS)
+        way_rows = (slice(0, CHUNKS), slice(32, 32 + 2 * CHUNKS), slice(64, 64 + 2 * CHUNKS))
+        for w in (1, 2, 0):
+            nc.sync.dma_start(turns[way_rows[w]], by_row[CHUNKS:] if w else by_row[0:CHUNKS])
 
         early = held.tile([P, 1], F32, name="early")
         nc.vector.memset(early[:], 0.0)
@@ -43,81 +44,100 @@ def tile_butterflymodule_kernel(tc, base, data, angles, offs, out):
         offsets = held.tile([P, N // 16], U16, name="offsets")
         nc.sync.dma_start(offsets[:], offs)
 
-        fresh, windows = [], []
-        for r in range(BLOCKS):
-            fresh.append(rows.tile([P, N], F32, name="fresh"))
-            nc.sync.dma_start(fresh[r][:], data[r * P : (r + 1) * P, :])
-        for r in range(BLOCKS):
-            windows.append(rows.tile([P, WIDE], F32, name="window"))
-            nc.sync.dma_start(windows[r][:], base[r * P : (r + 1) * P, :])
+        fresh = [rows.tile([P, N], F32, name="fresh") for r in range(BLOCKS)]
+        windows = [rows.tile([P, WIDE], F32, name="window") for r in range(BLOCKS)]
+        for r in range(BLOCKS + AHEAD - 1):
+            if r < BLOCKS:
+                nc.sync.dma_start(fresh[r][:], data[r * P : (r + 1) * P, :])
+            if r >= AHEAD - 1:
+                w = r - (AHEAD - 1)
+                nc.sync.dma_start(windows[w][:], base[w * P : (w + 1) * P, :])
 
         identity = held.tile([P, P], F32, name="identity")
         make_identity(nc, identity[:])
-        own_group = held.tile([P, P // GROUP], F32, name="own_group")
-        nc.vector.reduce_sum(own_group[:], identity[:].rearrange("k (g d) -> k g d", d=GROUP), axis=mybir.AxisListType.X)
-        signs = held.tile([P, 2, GROUP], F32, name="signs")
-        nc.vector.memset(signs[:], 1.0)
-        nc.vector.memset(signs[:, 1, 0:GROUP:2], -1.0)
-        signed_group = held.tile([P, 2, P], F32, name="signed_group")
-        nc.vector.tensor_tensor(
-            signed_group[:].rearrange("k t (g d) -> k t g d", d=GROUP),
-            own_group[:].unsqueeze(1).unsqueeze(3).broadcast_to([P, 2, P // GROUP, GROUP]),
-            signs[:].unsqueeze(2).broadcast_to([P, 2, P // GROUP, GROUP]),
-            MULT,
-        )
 
         place = held.tile([P, GROUP], F32, name="place")
         nc.vector.reduce_sum(place[:], identity[:].rearrange("k (g d) -> k d g", d=GROUP), axis=mybir.AxisListType.X)
-        high = held.tile([P, 2], F32, name="high")
-        nc.vector.reduce_sum(high[:], place[:].rearrange("k (h e) -> k h e", e=2), axis=mybir.AxisListType.X)
-        pick = held.tile([P, 2, 2, GROUP, 2], F32, name="pick")
-        nc.vector.memset(pick[:], 0.0)
-        by_low = place[:].rearrange("k (x b) -> k b x", b=2)
-        both = [P, 2, 2]
-        first_cos = pick[:, COS, 0].rearrange("k (a b) x -> k a b x", b=2)
-        first_sin = pick[:, SINE, 0].rearrange("k (a b) x -> k a b x", b=2)
-        nc.vector.tensor_copy(first_cos, by_low.unsqueeze(1).broadcast_to([P, 2, 2, 2]))
-        nc.vector.tensor_scalar_mul(first_sin[:, :, 0], by_low[:, 1].unsqueeze(1).broadcast_to(both), -1.0)
-        nc.vector.tensor_copy(first_sin[:, :, 1], by_low[:, 0].unsqueeze(1).broadcast_to(both))
-        second_cos = pick[:, COS, 1].rearrange("k (a b) x -> k a (b x)", b=2)[:, :, 0:4:3]
-        second_sin = pick[:, SINE, 1].rearrange("k (a b) x -> k a (b x)", b=2)[:, :, 0:4:3]
-        nc.vector.tensor_copy(second_cos, high[:].unsqueeze(2).broadcast_to(both))
-        nc.vector.tensor_scalar_mul(second_sin[:, 0], high[:, 1:2].broadcast_to([P, 2]), -1.0)
-        nc.vector.tensor_copy(second_sin[:, 1], high[:, 0:1].broadcast_to([P, 2]))
+        bits = held.tile([P, 2, 2], F32, name="bits")
+        nc.vector.reduce_sum(bits[:, 0], place[:].rearrange("k (h e) -> k e h", e=2), axis=mybir.AxisListType.X)
+        nc.vector.reduce_sum(bits[:, 1], place[:].rearrange("k (h e) -> k h e", e=2), axis=mybir.AxisListType.X)
+        phases = held.tile([P, WAYS, 2, CHUNKS, 2], F32, name="phases")
+        nc.gpsimd.memset(phases[:], 0.0)
+        nc.gpsimd.memset(phases[:, :, 1, :, 1], -math.pi / 2)
+        for turned_bit, ways in enumerate((slice(0, 1), slice(1, WAYS))):
+            for j in range(2):
+                there = phases[:, ways, 0, :, j]
+                nc.vector.tensor_scalar_mul(
+                    there,
+                    bits[:, turned_bit, 1 - j : 2 - j].unsqueeze(2).broadcast_to([P, ways.stop - ways.start, CHUNKS]),
+                    (1 - 2 * j) * math.pi / 2,
+                )
+        repeated = held.tile([P, P], F32, name="repeated")
+        nc.vector.memset(repeated[:], 0.0)
 
-        sines = in_turn.tile([P, LAYERS, CHUNKS, 2], F32, name="sines", tag="turn")
-        cosines = in_turn.tile([P, LAYERS, CHUNKS, 2], F32, name="cosines", tag="turn")
-        minus_size = held.tile([P, LAYERS, CHUNKS, 2], F32, name="minus_size")
-        nc.scalar.activation(sines[:], angle, SIN)
-        nc.vector.scalar_tensor_tensor(minus_size[:], angle, -1.0, angle, MULT, MIN)
-        nc.scalar.activation(cosines[:], minus_size[:], SIN, bias=math.pi / 2)
-
-        terms = held.tile([P, 2, 2, CHUNKS, GROUP, 2], F32, name="terms")
-        for f, function in ((SINE, sines), (COS, cosines)):
-            nc.vector.tensor_tensor(
-                terms[:, f],
-                function[:, 0:2].unsqueeze(3).broadcast_to([P, 2, CHUNKS, GROUP, 2]),
-                pick[:, f].unsqueeze(2).broadcast_to([P, 2, CHUNKS, GROUP, 2]),
-                MULT,
-            )
-        factor = held.tile([P, 2, CHUNKS * GROUP], F32, name="factor")
-        nc.vector.reduce_sum(
-            factor[:].rearrange("k l j -> k (l j)"),
-            terms[:].rearrange("k f l c j x -> k (l c j) f x"),
-            axis=mybir.AxisListType.XY,
+        own_group = held.tile([P, GROUPS], F32, name="own_group")
+        nc.vector.reduce_sum(own_group[:], identity[:].rearrange("k (g d) -> k g d", d=GROUP), axis=mybir.AxisListType.X)
+        signs = held.tile([P, 2, GROUP], F32, name="signs")
+        nc.gpsimd.memset(signs[:], 1.0)
+        nc.gpsimd.memset(signs[:, 1, 0:GROUP:2], -1.0)
+        signed_group = held.tile([P, 2, P], F32, name="signed_group")
+        nc.gpsimd.tensor_tensor(
+            signed_group[:].rearrange("k t (g d) -> k t g d", d=GROUP),
+            own_group[:].unsqueeze(1).unsqueeze(3).broadcast_to([P, 2, GROUPS, GROUP]),
+            signs[:].unsqueeze(2).broadcast_to([P, 2, GROUPS, GROUP]),
+            MULT,
         )
+
+        for w, copy in enumerate((nc.vector.tensor_copy, nc.vector.tensor_copy, nc.scalar.copy)):
+            pairs = turns[way_rows[w]].rearrange("i (g x) -> i g x", x=2)
+            count = way_rows[w].stop - way_rows[w].start
+            if w == 0:
+                copy(
+                    repeated[way_rows[w]].rearrange("i (g h e) -> i g h e", h=2, e=2),
+                    pairs.unsqueeze(3).broadcast_to([count, GROUPS, 2, 2]),
+                )
+            else:
+                copy(
+                    repeated[way_rows[w]].rearrange("i (g m) -> i g m", m=GROUP),
+                    pairs[:, :, w - 1 : w].broadcast_to([count, GROUPS, GROUP]),
+                )
+        handed = banks.tile([P, P], F32, name="handed", tag="bank")
+        nc.tensor.transpose(handed[:], repeated[:], identity[:])
+        shifted = held.tile([P, WAYS, 2 * CHUNKS, 2], F32, name="shifted")
+        nc.vector.tensor_tensor(
+            shifted[:],
+            handed[:].rearrange("k (w s) -> k w s", s=32)[:, 0:WAYS, 0 : 2 * CHUNKS].unsqueeze(3).broadcast_to([P, WAYS, 2 * CHUNKS, 2]),
+            phases[:].rearrange("k w l c j -> k w (l c) j"),
+            ADD,
+        )
+
+        minus_size = held.tile([P, WAYS, 2, CHUNKS, 2], F32, name="minus_size")
+        factors = in_turn.tile([P, WAYS, 2, CHUNKS, 2], F32, name="factors", tag="turn")
+        flat = [tile[:].rearrange("k w l c j -> k (w l c j)") for tile in (minus_size, factors)]
+        s = shifted[:].rearrange("k w s j -> k (w s j)")
+        nc.vector.scalar_tensor_tensor(flat[0], s, -1.0, s, MULT, MIN)
+        nc.scalar.activation(flat[1], flat[0], SIN, bias=math.pi / 2)
+
         turned = held.tile([P, CHUNKS, 2, 2], F32, name="turned")
-        nc.vector.tensor_tensor(turned[:].rearrange("k c a b -> k (c a b)"), factor[:, 0], factor[:, 1], MULT)
+        for_both = [P, CHUNKS, 2, 2]
+        nc.vector.tensor_tensor(
+            turned[:],
+            factors[:, 0, 0].unsqueeze(2).broadcast_to(for_both),
+            factors[:, 1:WAYS, 0].rearrange("k b c a -> k c a b"),
+            MULT,
+        )
 
         entries = held.tile([P, 2, CHUNKS, 2, 2], F32, name="entries")
-        for_both = [P, CHUNKS, 2, 2]
-        nc.vector.tensor_tensor(entries[:, 0], turned[:], cosines[:, 2].unsqueeze(3).broadcast_to(for_both), MULT)
-        nc.vector.tensor_tensor(entries[:, 1], turned[:, :, :, ::-1], sines[:, 2].unsqueeze(3).broadcast_to(for_both), MULT)
+        cosines, sines = (
+            factors[:, 1:WAYS, 1, :, f].rearrange("k a c -> k c a").unsqueeze(3).broadcast_to(for_both) for f in range(2)
+        )
+        nc.vector.tensor_tensor(entries[:, 0], turned[:], cosines, MULT)
+        nc.vector.tensor_tensor(entries[:, 1], turned[:, :, :, ::-1], sines, MULT)
 
         matrix = held.tile([P, CHUNKS, 2, P], F32, name="matrix")
-        spread = [P, 2, P // GROUP, GROUP]
+        spread = [P, 2, GROUPS, GROUP]
         for c in range(CHUNKS):
-            nc.vector.tensor_tensor(
+            (nc.gpsimd if c == CHUNKS - 1 else nc.vector).tensor_tensor(
                 matrix[:, c].rearrange("k t (g d) -> k t g d", d=GROUP),
                 entries[:, :, c].rearrange("k t a b -> k t (a b)").unsqueeze(2).broadcast_to(spread),
                 signed_group[:].rearrange("k t (g d) -> k t g d", d=GROUP),

@@ -29,7 +29,8 @@ def tile_butterflymodule_kernel(tc, base, data, angles, offs, out):
         tc.tile_pool(name="held", bufs=1) as held,
         tc.tile_pool(name="rows", bufs=BLOCKS) as rows,
         tc.tile_pool(name="in_turn", bufs=BLOCKS + 2) as in_turn,
-        tc.psum_pool(name="banks", bufs=8) as banks,
+        tc.psum_pool(name="lead", bufs=1) as lead,
+        tc.psum_pool(name="banks", bufs=7) as banks,
     ):
         turns = held.tile([P, 2 * GROUPS], F32, name="turns")
         by_row = angles.rearrange("l (c u) -> (l c) u", c=CHUNKS)
@@ -46,12 +47,12 @@ def tile_butterflymodule_kernel(tc, base, data, angles, offs, out):
 
         fresh = [rows.tile([P, N], F32, name="fresh") for r in range(BLOCKS)]
         windows = [rows.tile([P, WIDE], F32, name="window") for r in range(BLOCKS)]
-        for r in range(BLOCKS + AHEAD - 1):
-            if r < BLOCKS:
+        for first in range(0, BLOCKS, AHEAD):
+            two = range(first, first + AHEAD)
+            for r in two:
                 nc.sync.dma_start(fresh[r][:], data[r * P : (r + 1) * P, :])
-            if r >= AHEAD - 1:
-                w = r - (AHEAD - 1)
-                nc.sync.dma_start(windows[w][:], base[w * P : (w + 1) * P, :])
+            for r in two:
+                nc.sync.dma_start(windows[r][:], base[r * P : (r + 1) * P, :])
 
         identity = held.tile([P, P], F32, name="identity")
         make_identity(nc, identity[:])
@@ -101,7 +102,7 @@ def tile_butterflymodule_kernel(tc, base, data, angles, offs, out):
                     repeated[way_rows[w]].rearrange("i (g m) -> i g m", m=GROUP),
                     pairs[:, :, w - 1 : w].broadcast_to([count, GROUPS, GROUP]),
                 )
-        handed = banks.tile([P, P], F32, name="handed", tag="bank")
+        handed = lead.tile([P, P], F32, name="handed", tag="lead")
         nc.tensor.transpose(handed[:], repeated[:], identity[:])
         shifted = held.tile([P, WAYS, 2 * CHUNKS, 2], F32, name="shifted")
         nc.vector.tensor_tensor(
@@ -147,15 +148,20 @@ def tile_butterflymodule_kernel(tc, base, data, angles, offs, out):
         flipped = []
 
         def flip(r):
-            flipped_bank = banks.tile([P, N], F32, name="flipped_bank", tag="bank")
-            for c in range(CHUNKS):
-                block = fresh[r][:, c * P : (c + 1) * P]
-                if r == AHEAD - 1:
-                    nc.tensor.matmul(flipped_bank[:, c * P : (c + 1) * P], lhsT=block, rhs=identity[:], start=True, stop=True)
-                else:
-                    nc.tensor.transpose(flipped_bank[:, c * P : (c + 1) * P], block, identity[:])
             flipped.append(in_turn.tile([P, N], F32, name="flipped", tag="turn"))
-            nc.scalar.copy(flipped[r][:], flipped_bank[:])
+            for half in range(2):
+                pool, tag = (lead, "lead") if (r, half) == (1, 0) else (banks, "bank")
+                flipped_bank = pool.tile([P, 2, P], F32, name="flipped_bank", tag=tag)
+                for e in range(2):
+                    c = 2 * half + e
+                    block = fresh[r][:, c * P : (c + 1) * P]
+                    if (r, half) == (1, 0):
+                        nc.tensor.matmul(flipped_bank[:, e], lhsT=block, rhs=identity[:], start=True, stop=True)
+                    else:
+                        nc.tensor.transpose(flipped_bank[:, e], block, identity[:])
+                nc.scalar.copy(
+                    flipped[r][:, 2 * half * P : 2 * (half + 1) * P], flipped_bank[:].rearrange("k e j -> k (e j)")
+                )
 
         for r in range(AHEAD):
             flip(r)
@@ -163,7 +169,7 @@ def tile_butterflymodule_kernel(tc, base, data, angles, offs, out):
             products = rows.tile([P, 2, N], F32, name="products")
             for c in range(CHUNKS):
                 here = slice(c * P, (c + 1) * P)
-                if r == 0:
+                if r == 0 and c == CHUNKS - 1:
                     for t, copy_out in enumerate((nc.scalar.copy, nc.vector.tensor_copy)):
                         half_bank = banks.tile([P, P], F32, name="half_bank", tag="bank")
                         nc.tensor.matmul(half_bank[:], lhsT=flipped[r][:, here], rhs=matrix[:, c, t], start=True, stop=True)
@@ -171,7 +177,8 @@ def tile_butterflymodule_kernel(tc, base, data, angles, offs, out):
                 else:
                     bank = banks.tile([P, 2, P], F32, name="bank", tag="bank")
                     nc.tensor.matmul(bank[:], lhsT=flipped[r][:, here], rhs=matrix[:, c], start=True, stop=True)
-                    nc.scalar.copy(products[:, :, here], bank[:])
+                    copy_out = nc.vector.tensor_copy if r == 0 and c % 2 else nc.scalar.copy
+                    copy_out(products[:, :, here], bank[:])
             if r + AHEAD < BLOCKS:
                 flip(r + AHEAD)
 

@@ -7,10 +7,11 @@ F32 = mybir.dt.float32
 U16 = mybir.dt.uint16
 MULT = mybir.AluOpType.mult
 ADD = mybir.AluOpType.add
-MIN = mybir.AluOpType.min
 SIN = mybir.ActivationFunctionType.Sin
+ABS = mybir.ActivationFunctionType.Abs
 
 P = 128
+QUARTER = 32
 ROWS, WIDE, N = 512, 2048, 512
 STRIDES = (1, 2, 1)
 LAYERS = len(STRIDES)
@@ -19,7 +20,6 @@ GROUPS = P // GROUP
 BLOCKS = ROWS // P
 AHEAD = 2
 CHUNKS = N // P
-WAYS = 3
 FLOPS = LAYERS * ROWS * (N // 2) * 6
 
 
@@ -29,14 +29,15 @@ def tile_butterflymodule_kernel(tc, base, data, angles, offs, out):
         tc.tile_pool(name="held", bufs=1) as held,
         tc.tile_pool(name="rows", bufs=BLOCKS) as rows,
         tc.tile_pool(name="in_turn", bufs=BLOCKS + 2) as in_turn,
-        tc.psum_pool(name="lead", bufs=1) as lead,
-        tc.psum_pool(name="banks", bufs=7) as banks,
+        tc.psum_pool(name="banks", bufs=8) as banks,
     ):
         turns = held.tile([P, 2 * GROUPS], F32, name="turns")
-        by_row = angles.rearrange("l (c u) -> (l c) u", c=CHUNKS)
-        way_rows = (slice(0, CHUNKS), slice(32, 32 + 2 * CHUNKS), slice(64, 64 + 2 * CHUNKS))
-        for w in (1, 2, 0):
-            nc.sync.dma_start(turns[way_rows[w]], by_row[CHUNKS:] if w else by_row[0:CHUNKS])
+        rows_of = angles.rearrange("l (c u) -> (l c) u", c=CHUNKS)
+        late_rows = [slice(QUARTER * x, QUARTER * x + 2 * CHUNKS) for x in range(2)]
+        first_rows = slice(2 * QUARTER, 2 * QUARTER + CHUNKS)
+        for x in range(2):
+            nc.sync.dma_start(turns[late_rows[x]], rows_of[CHUNKS:])
+        nc.sync.dma_start(turns[first_rows], rows_of[0:CHUNKS])
 
         early = held.tile([P, 1], F32, name="early")
         nc.vector.memset(early[:], 0.0)
@@ -47,8 +48,8 @@ def tile_butterflymodule_kernel(tc, base, data, angles, offs, out):
 
         fresh = [rows.tile([P, N], F32, name="fresh") for r in range(BLOCKS)]
         windows = [rows.tile([P, WIDE], F32, name="window") for r in range(BLOCKS)]
-        for first in range(0, BLOCKS, AHEAD):
-            two = range(first, first + AHEAD)
+        for lowest in range(0, BLOCKS, AHEAD):
+            two = range(lowest, lowest + AHEAD)
             for r in two:
                 nc.sync.dma_start(fresh[r][:], data[r * P : (r + 1) * P, :])
             for r in two:
@@ -57,27 +58,20 @@ def tile_butterflymodule_kernel(tc, base, data, angles, offs, out):
         identity = held.tile([P, P], F32, name="identity")
         make_identity(nc, identity[:])
 
-        place = held.tile([P, GROUP], F32, name="place")
-        nc.vector.reduce_sum(place[:], identity[:].rearrange("k (g d) -> k d g", d=GROUP), axis=mybir.AxisListType.X)
-        bits = held.tile([P, 2, 2], F32, name="bits")
-        nc.vector.reduce_sum(bits[:, 0], place[:].rearrange("k (h e) -> k e h", e=2), axis=mybir.AxisListType.X)
-        nc.vector.reduce_sum(bits[:, 1], place[:].rearrange("k (h e) -> k h e", e=2), axis=mybir.AxisListType.X)
-        phases = held.tile([P, WAYS, 2, CHUNKS, 2], F32, name="phases")
-        nc.gpsimd.memset(phases[:], 0.0)
-        nc.gpsimd.memset(phases[:, :, 1, :, 1], -math.pi / 2)
-        for turned_bit, ways in enumerate((slice(0, 1), slice(1, WAYS))):
-            for j in range(2):
-                there = phases[:, ways, 0, :, j]
-                nc.vector.tensor_scalar_mul(
-                    there,
-                    bits[:, turned_bit, 1 - j : 2 - j].unsqueeze(2).broadcast_to([P, ways.stop - ways.start, CHUNKS]),
-                    (1 - 2 * j) * math.pi / 2,
-                )
-        repeated = held.tile([P, P], F32, name="repeated")
-        nc.vector.memset(repeated[:], 0.0)
+        shift = held.tile([P, 2, 2], F32, name="shift")
+        nc.vector.memset(shift[:], 0.0)
+        nc.vector.memset(shift[first_rows, :, 1], math.pi / 2)
+        for x in range(2):
+            layer_1 = slice(late_rows[x].start, late_rows[x].start + CHUNKS)
+            nc.vector.memset(shift[layer_1, 1], math.pi / 2)
+        shifted = held.tile([P, P], F32, name="shifted")
+        nc.vector.memset(shifted[:], 0.0)
 
+        pair_sums = held.tile([P, GROUPS, 2], F32, name="pair_sums")
         own_group = held.tile([P, GROUPS], F32, name="own_group")
-        nc.vector.reduce_sum(own_group[:], identity[:].rearrange("k (g d) -> k g d", d=GROUP), axis=mybir.AxisListType.X)
+        by_fours = identity[:].rearrange("k (g d) -> k g d", d=GROUP)
+        nc.gpsimd.tensor_tensor(pair_sums[:], by_fours[:, :, 0:2], by_fours[:, :, 2:4], ADD)
+        nc.gpsimd.tensor_tensor(own_group[:], pair_sums[:, :, 0], pair_sums[:, :, 1], ADD)
         signs = held.tile([P, 2, GROUP], F32, name="signs")
         nc.gpsimd.memset(signs[:], 1.0)
         nc.gpsimd.memset(signs[:, 1, 0:GROUP:2], -1.0)
@@ -89,69 +83,68 @@ def tile_butterflymodule_kernel(tc, base, data, angles, offs, out):
             MULT,
         )
 
-        for w, copy in enumerate((nc.vector.tensor_copy, nc.vector.tensor_copy, nc.scalar.copy)):
-            pairs = turns[way_rows[w]].rearrange("i (g x) -> i g x", x=2)
-            count = way_rows[w].stop - way_rows[w].start
-            if w == 0:
-                copy(
-                    repeated[way_rows[w]].rearrange("i (g h e) -> i g h e", h=2, e=2),
-                    pairs.unsqueeze(3).broadcast_to([count, GROUPS, 2, 2]),
-                )
-            else:
-                copy(
-                    repeated[way_rows[w]].rearrange("i (g m) -> i g m", m=GROUP),
-                    pairs[:, :, w - 1 : w].broadcast_to([count, GROUPS, GROUP]),
-                )
-        handed = lead.tile([P, P], F32, name="handed", tag="lead")
-        nc.tensor.transpose(handed[:], repeated[:], identity[:])
-        shifted = held.tile([P, WAYS, 2 * CHUNKS, 2], F32, name="shifted")
+        by_place = [2 * CHUNKS, GROUPS, GROUP]
+        for x in range(2):
+            nc.vector.tensor_tensor(
+                shifted[late_rows[x]].rearrange("i (g m) -> i g m", m=GROUP),
+                turns[late_rows[x], x : 2 * GROUPS : 2].unsqueeze(2).broadcast_to(by_place),
+                shift[late_rows[x]].rearrange("i h e -> i (h e)").unsqueeze(1).broadcast_to(by_place),
+                ADD,
+            )
+        by_bits = [CHUNKS, GROUPS, 2, 2]
         nc.vector.tensor_tensor(
-            shifted[:],
-            handed[:].rearrange("k (w s) -> k w s", s=32)[:, 0:WAYS, 0 : 2 * CHUNKS].unsqueeze(3).broadcast_to([P, WAYS, 2 * CHUNKS, 2]),
-            phases[:].rearrange("k w l c j -> k w (l c) j"),
+            shifted[first_rows].rearrange("i (g h e) -> i g h e", h=2, e=2),
+            turns[first_rows].rearrange("i (g x) -> i g x", x=2).unsqueeze(3).broadcast_to(by_bits),
+            shift[first_rows].unsqueeze(1).broadcast_to(by_bits),
             ADD,
         )
+        handed = banks.tile([P, P], F32, name="handed", tag="bank")
+        nc.tensor.transpose(handed[:], shifted[:], identity[:])
 
-        minus_size = held.tile([P, WAYS, 2, CHUNKS, 2], F32, name="minus_size")
-        factors = in_turn.tile([P, WAYS, 2, CHUNKS, 2], F32, name="factors", tag="turn")
-        flat = [tile[:].rearrange("k w l c j -> k (w l c j)") for tile in (minus_size, factors)]
-        s = shifted[:].rearrange("k w s j -> k (w s j)")
-        nc.vector.scalar_tensor_tensor(flat[0], s, -1.0, s, MULT, MIN)
-        nc.scalar.activation(flat[1], flat[0], SIN, bias=math.pi / 2)
+        by_new_bit = [P, 2, 3, 2 * CHUNKS]
+        size = in_turn.tile(by_new_bit, F32, name="size", tag="turn")
+        factors = in_turn.tile(by_new_bit, F32, name="factors", tag="turn")
+        used = handed[:].rearrange("k (q i) -> k q i", i=QUARTER)[:, 0:3, 0 : 2 * CHUNKS]
+        for j in range(2):
+            nc.scalar.activation(size[:, j], used, ABS, bias=(0.0, -math.pi / 2)[j])
+        nc.scalar.activation(factors[:], size[:], SIN, bias=math.pi / 2, scale=-1.0)
+        first = factors[:, :, 2, 0:CHUNKS].rearrange("k b c -> k c b")
+        later = factors[:, :, 0:2].rearrange("k j x (l c) -> k j x l c", c=CHUNKS)
 
         turned = held.tile([P, CHUNKS, 2, 2], F32, name="turned")
         for_both = [P, CHUNKS, 2, 2]
         nc.vector.tensor_tensor(
-            turned[:],
-            factors[:, 0, 0].unsqueeze(2).broadcast_to(for_both),
-            factors[:, 1:WAYS, 0].rearrange("k b c a -> k c a b"),
-            MULT,
+            turned[:], first.unsqueeze(2).broadcast_to(for_both), later[:, :, :, 0].rearrange("k a b c -> k c a b"), MULT
         )
 
         entries = held.tile([P, 2, CHUNKS, 2, 2], F32, name="entries")
         cosines, sines = (
-            factors[:, 1:WAYS, 1, :, f].rearrange("k a c -> k c a").unsqueeze(3).broadcast_to(for_both) for f in range(2)
+            later[:, f, :, 1].rearrange("k a c -> k c a").unsqueeze(3).broadcast_to(for_both) for f in range(2)
         )
         nc.vector.tensor_tensor(entries[:, 0], turned[:], cosines, MULT)
         nc.vector.tensor_tensor(entries[:, 1], turned[:, :, :, ::-1], sines, MULT)
 
         matrix = held.tile([P, CHUNKS, 2, P], F32, name="matrix")
-        spread = [P, 2, GROUPS, GROUP]
-        for c in range(CHUNKS):
-            (nc.gpsimd if c == CHUNKS - 1 else nc.vector).tensor_tensor(
-                matrix[:, c].rearrange("k t (g d) -> k t g d", d=GROUP),
-                entries[:, :, c].rearrange("k t a b -> k t (a b)").unsqueeze(2).broadcast_to(spread),
-                signed_group[:].rearrange("k t (g d) -> k t g d", d=GROUP),
+        def spread_out(engine, c, products):
+            spread = [P, products.stop - products.start, GROUPS, GROUP]
+            engine.tensor_tensor(
+                matrix[:, c, products].rearrange("k t (g d) -> k t g d", d=GROUP),
+                entries[:, products, c].rearrange("k t a b -> k t (a b)").unsqueeze(2).broadcast_to(spread),
+                signed_group[:, products].rearrange("k t (g d) -> k t g d", d=GROUP),
                 MULT,
             )
+
+        for t in range(2):
+            spread_out(nc.vector, 0, slice(t, t + 1))
+        for c in range(1, CHUNKS):
+            spread_out(nc.gpsimd if c == CHUNKS - 1 else nc.vector, c, slice(0, 2))
 
         flipped = []
 
         def flip(r):
             flipped.append(in_turn.tile([P, N], F32, name="flipped", tag="turn"))
             for half in range(2):
-                pool, tag = (lead, "lead") if (r, half) == (1, 0) else (banks, "bank")
-                flipped_bank = pool.tile([P, 2, P], F32, name="flipped_bank", tag=tag)
+                flipped_bank = banks.tile([P, 2, P], F32, name="flipped_bank", tag="bank")
                 for e in range(2):
                     c = 2 * half + e
                     block = fresh[r][:, c * P : (c + 1) * P]
@@ -169,7 +162,7 @@ def tile_butterflymodule_kernel(tc, base, data, angles, offs, out):
             products = rows.tile([P, 2, N], F32, name="products")
             for c in range(CHUNKS):
                 here = slice(c * P, (c + 1) * P)
-                if r == 0 and c == CHUNKS - 1:
+                if r == 0 and c in (0, CHUNKS - 1):
                     for t, copy_out in enumerate((nc.scalar.copy, nc.vector.tensor_copy)):
                         half_bank = banks.tile([P, P], F32, name="half_bank", tag="bank")
                         nc.tensor.matmul(half_bank[:], lhsT=flipped[r][:, here], rhs=matrix[:, c, t], start=True, stop=True)

@@ -7,6 +7,8 @@ F32 = mybir.dt.float32
 U16 = mybir.dt.uint16
 MULT = mybir.AluOpType.mult
 ADD = mybir.AluOpType.add
+IS_GE = mybir.AluOpType.is_ge
+IS_LE = mybir.AluOpType.is_le
 SIN = mybir.ActivationFunctionType.Sin
 ABS = mybir.ActivationFunctionType.Abs
 
@@ -55,6 +57,25 @@ def tile_butterflymodule_kernel(tc, base, data, angles, offs, out):
             for r in two:
                 nc.sync.dma_start(windows[r][:], base[r * P : (r + 1) * P, :])
 
+        offset = held.tile([P, GROUPS], F32, name="offset")
+        nc.gpsimd.iota(
+            offset[:], pattern=[[-GROUP, GROUPS]], base=0, channel_multiplier=1, allow_small_or_imprecise_dtypes=True
+        )
+        not_before = held.tile([P, GROUPS], F32, name="not_before")
+        own_group = held.tile([P, GROUPS], F32, name="own_group")
+        nc.vector.tensor_single_scalar(not_before[:], offset[:], 0.0, op=IS_GE)
+        nc.vector.scalar_tensor_tensor(own_group[:], offset[:], GROUP - 1.0, not_before[:], IS_LE, MULT)
+        signs = held.tile([P, 2, GROUP], F32, name="signs")
+        nc.vector.memset(signs[:], 1.0)
+        nc.vector.memset(signs[:, 1, 0:GROUP:2], -1.0)
+        signed_group = held.tile([P, 2, P], F32, name="signed_group")
+        nc.vector.tensor_tensor(
+            signed_group[:].rearrange("k t (g d) -> k t g d", d=GROUP),
+            own_group[:].unsqueeze(1).unsqueeze(3).broadcast_to([P, 2, GROUPS, GROUP]),
+            signs[:].unsqueeze(2).broadcast_to([P, 2, GROUPS, GROUP]),
+            MULT,
+        )
+
         identity = held.tile([P, P], F32, name="identity")
         make_identity(nc, identity[:])
 
@@ -66,22 +87,6 @@ def tile_butterflymodule_kernel(tc, base, data, angles, offs, out):
             nc.vector.memset(shift[layer_1, 1], math.pi / 2)
         shifted = held.tile([P, P], F32, name="shifted")
         nc.vector.memset(shifted[:], 0.0)
-
-        pair_sums = held.tile([P, GROUPS, 2], F32, name="pair_sums")
-        own_group = held.tile([P, GROUPS], F32, name="own_group")
-        by_fours = identity[:].rearrange("k (g d) -> k g d", d=GROUP)
-        nc.gpsimd.tensor_tensor(pair_sums[:], by_fours[:, :, 0:2], by_fours[:, :, 2:4], ADD)
-        nc.gpsimd.tensor_tensor(own_group[:], pair_sums[:, :, 0], pair_sums[:, :, 1], ADD)
-        signs = held.tile([P, 2, GROUP], F32, name="signs")
-        nc.gpsimd.memset(signs[:], 1.0)
-        nc.gpsimd.memset(signs[:, 1, 0:GROUP:2], -1.0)
-        signed_group = held.tile([P, 2, P], F32, name="signed_group")
-        nc.gpsimd.tensor_tensor(
-            signed_group[:].rearrange("k t (g d) -> k t g d", d=GROUP),
-            own_group[:].unsqueeze(1).unsqueeze(3).broadcast_to([P, 2, GROUPS, GROUP]),
-            signs[:].unsqueeze(2).broadcast_to([P, 2, GROUPS, GROUP]),
-            MULT,
-        )
 
         by_place = [2 * CHUNKS, GROUPS, GROUP]
         for x in range(2):
@@ -125,9 +130,9 @@ def tile_butterflymodule_kernel(tc, base, data, angles, offs, out):
         nc.vector.tensor_tensor(entries[:, 1], turned[:, :, :, ::-1], sines, MULT)
 
         matrix = held.tile([P, CHUNKS, 2, P], F32, name="matrix")
-        def spread_out(engine, c, products):
+        def spread_out(c, products):
             spread = [P, products.stop - products.start, GROUPS, GROUP]
-            engine.tensor_tensor(
+            nc.vector.tensor_tensor(
                 matrix[:, c, products].rearrange("k t (g d) -> k t g d", d=GROUP),
                 entries[:, products, c].rearrange("k t a b -> k t (a b)").unsqueeze(2).broadcast_to(spread),
                 signed_group[:, products].rearrange("k t (g d) -> k t g d", d=GROUP),
@@ -135,9 +140,9 @@ def tile_butterflymodule_kernel(tc, base, data, angles, offs, out):
             )
 
         for t in range(2):
-            spread_out(nc.vector, 0, slice(t, t + 1))
+            spread_out(0, slice(t, t + 1))
         for c in range(1, CHUNKS):
-            spread_out(nc.gpsimd if c == CHUNKS - 1 else nc.vector, c, slice(0, 2))
+            spread_out(c, slice(0, 2))
 
         flipped = []
 

@@ -161,9 +161,10 @@ def tile_butterflymodule_kernel(tc, base, data, angles, offs, out):
                     flipped[r][:, 2 * half * P : 2 * (half + 1) * P], flipped_bank[:].rearrange("k e j -> k (e j)")
                 )
 
-        for r in range(AHEAD):
-            flip(r)
         for r in range(BLOCKS):
+            if r % AHEAD == 0:
+                for ahead in range(r, r + AHEAD):
+                    flip(ahead)
             products = rows.tile([P, 2, N], F32, name="products")
             for c in range(CHUNKS):
                 here = slice(c * P, (c + 1) * P)
@@ -177,8 +178,6 @@ def tile_butterflymodule_kernel(tc, base, data, angles, offs, out):
                     nc.tensor.matmul(bank[:], lhsT=flipped[r][:, here], rhs=matrix[:, c], start=True, stop=True)
                     copy_out = nc.vector.tensor_copy if r == 0 and c % 2 else nc.scalar.copy
                     copy_out(products[:, :, here], bank[:])
-            if r + AHEAD < BLOCKS:
-                flip(r + AHEAD)
 
             nc.vector.tensor_tensor(windows[r][:].indirect(offsets[:]), products[:, 0], products[:, 1], ADD)
             nc.sync.dma_start(out[r * P : (r + 1) * P, :], windows[r][:])

@@ -22,6 +22,7 @@ GROUPS = P // GROUP
 BLOCKS = ROWS // P
 AHEAD = 2
 CHUNKS = N // P
+MATMUL_FLIPS = ((0, 2), (0, 3), (1, 0))
 FLOPS = LAYERS * ROWS * (N // 2) * 6
 
 
@@ -153,7 +154,7 @@ def tile_butterflymodule_kernel(tc, base, data, angles, offs, out):
                 for e in range(2):
                     c = 2 * half + e
                     block = fresh[r][:, c * P : (c + 1) * P]
-                    if (r, half) == (1, 0):
+                    if (r, c) in MATMUL_FLIPS:
                         nc.tensor.matmul(flipped_bank[:, e], lhsT=block, rhs=identity[:], start=True, stop=True)
                     else:
                         nc.tensor.transpose(flipped_bank[:, e], block, identity[:])

@@ -22,7 +22,6 @@ GROUPS = P // GROUP
 BLOCKS = ROWS // P
 AHEAD = 2
 CHUNKS = N // P
-MATMUL_FLIPS = ((0, 2), (0, 3), (1, 0))
 FLOPS = LAYERS * ROWS * (N // 2) * 6
 
 
@@ -154,7 +153,7 @@ def tile_butterflymodule_kernel(tc, base, data, angles, offs, out):
                 for e in range(2):
                     c = 2 * half + e
                     block = fresh[r][:, c * P : (c + 1) * P]
-                    if (r, c) in MATMUL_FLIPS:
+                    if 2 <= r * CHUNKS + c < 5:
                         nc.tensor.matmul(flipped_bank[:, e], lhsT=block, rhs=identity[:], start=True, stop=True)
                     else:
                         nc.tensor.transpose(flipped_bank[:, e], block, identity[:])
@@ -170,7 +169,7 @@ def tile_butterflymodule_kernel(tc, base, data, angles, offs, out):
             for c in range(CHUNKS):
                 here = slice(c * P, (c + 1) * P)
                 if r == 0 and c in (0, CHUNKS - 1):
-                    for t, copy_out in enumerate((nc.scalar.copy, nc.vector.tensor_copy)):
+                    for t, copy_out in enumerate((nc.vector.tensor_copy, nc.scalar.copy)):
                         half_bank = banks.tile([P, P], F32, name="half_bank", tag="bank")
                         nc.tensor.matmul(half_bank[:], lhsT=flipped[r][:, here], rhs=matrix[:, c, t], start=True, stop=True)
                         copy_out(products[:, t, here], half_bank[:])

import math

import concourse.mybir as mybir
from concourse.masks import make_identity

F32 = mybir.dt.float32
U16 = mybir.dt.uint16
MULT = mybir.AluOpType.mult
ADD = mybir.AluOpType.add
IS_GE = mybir.AluOpType.is_ge
IS_LE = mybir.AluOpType.is_le
SIN = mybir.ActivationFunctionType.Sin
ABS = mybir.ActivationFunctionType.Abs

P = 128
QUARTER = 32
ROWS, WIDE, N = 512, 2048, 512
STRIDES = (1, 2, 1)
LAYERS = len(STRIDES)
GROUP = 4
GROUPS = P // GROUP
BLOCKS = ROWS // P
AHEAD = 2
CHUNKS = N // P
FLOPS = LAYERS * ROWS * (N // 2) * 6


def tile_butterflymodule_kernel(tc, base, data, angles, offs, out):
    nc = tc.nc
    with (
        tc.tile_pool(name="held", bufs=1) as held,
        tc.tile_pool(name="rows", bufs=BLOCKS) as rows,
        tc.tile_pool(name="in_turn", bufs=BLOCKS + 2) as in_turn,
        tc.psum_pool(name="banks", bufs=8) as banks,
    ):
        turns = held.tile([P, 2 * GROUPS], F32, name="turns")
        rows_of = angles.rearrange("l (c u) -> (l c) u", c=CHUNKS)
        late_rows = [slice(QUARTER * x, QUARTER * x + 2 * CHUNKS) for x in range(2)]
        first_rows = slice(2 * QUARTER, 2 * QUARTER + CHUNKS)
        for x in range(2):
            nc.sync.dma_start(turns[late_rows[x]], rows_of[CHUNKS:])
        nc.sync.dma_start(turns[first_rows], rows_of[0:CHUNKS])

        early = held.tile([P, 1], F32, name="early")
        nc.vector.memset(early[:], 0.0)
        nc.scalar.activation(early[:], early[:], SIN)

        offsets = held.tile([P, N // 16], U16, name="offsets")
        nc.sync.dma_start(offsets[:], offs)

        fresh = [rows.tile([P, N], F32, name="fresh") for r in range(BLOCKS)]
        windows = [rows.tile([P, WIDE], F32, name="window") for r in range(BLOCKS)]
        for lowest in range(0, BLOCKS, AHEAD):
            two = range(lowest, lowest + AHEAD)
            for r in two:
                nc.sync.dma_start(fresh[r][:], data[r * P : (r + 1) * P, :])
            for r in two:
                nc.sync.dma_start(windows[r][:], base[r * P : (r + 1) * P, :])

        offset = held.tile([P, GROUPS], F32, name="offset")
        nc.gpsimd.iota(
            offset[:], pattern=[[-GROUP, GROUPS]], base=0, channel_multiplier=1, allow_small_or_imprecise_dtypes=True
        )
        not_before = held.tile([P, GROUPS], F32, name="not_before")
        own_group = held.tile([P, GROUPS], F32, name="own_group")
        nc.vector.tensor_single_scalar(not_before[:], offset[:], 0.0, op=IS_GE)
        nc.vector.scalar_tensor_tensor(own_group[:], offset[:], GROUP - 1.0, not_before[:], IS_LE, MULT)
        signs = held.tile([P, 2, GROUP], F32, name="signs")
        nc.vector.memset(signs[:], 1.0)
        nc.vector.memset(signs[:, 1, 0:GROUP:2], -1.0)
        signed_group = held.tile([P, 2, P], F32, name="signed_group")
        nc.vector.tensor_tensor(
            signed_group[:].rearrange("k t (g d) -> k t g d", d=GROUP),
            own_group[:].unsqueeze(1).unsqueeze(3).broadcast_to([P, 2, GROUPS, GROUP]),
            signs[:].unsqueeze(2).broadcast_to([P, 2, GROUPS, GROUP]),
            MULT,
        )

        identity = held.tile([P, P], F32, name="identity")
        make_identity(nc, identity[:])

        shift = held.tile([P, 2, 2], F32, name="shift")
        nc.vector.memset(shift[:], 0.0)
        nc.vector.memset(shift[first_rows, :, 1], math.pi / 2)
        for x in range(2):
            layer_1 = slice(late_rows[x].start, late_rows[x].start + CHUNKS)
            nc.vector.memset(shift[layer_1, 1], math.pi / 2)
        shifted = held.tile([P, P], F32, name="shifted")
        nc.vector.memset(shifted[:], 0.0)

        by_place = [2 * CHUNKS, GROUPS, GROUP]
        for x in range(2):
            nc.vector.tensor_tensor(
                shifted[late_rows[x]].rearrange("i (g m) -> i g m", m=GROUP),
                turns[late_rows[x], x : 2 * GROUPS : 2].unsqueeze(2).broadcast_to(by_place),
                shift[late_rows[x]].rearrange("i h e -> i (h e)").unsqueeze(1).broadcast_to(by_place),
                ADD,
            )
        by_bits = [CHUNKS, GROUPS, 2, 2]
        nc.vector.tensor_tensor(
            shifted[first_rows].rearrange("i (g h e) -> i g h e", h=2, e=2),
            turns[first_rows].rearrange("i (g x) -> i g x", x=2).unsqueeze(3).broadcast_to(by_bits),
            shift[first_rows].unsqueeze(1).broadcast_to(by_bits),
            ADD,
        )
        handed = banks.tile([P, P], F32, name="handed", tag="bank")
        nc.tensor.transpose(handed[:], shifted[:], identity[:])

        by_new_bit = [P, 2, 3, 2 * CHUNKS]
        size = in_turn.tile(by_new_bit, F32, name="size", tag="turn")
        factors = in_turn.tile(by_new_bit, F32, name="factors", tag="turn")
        used = handed[:].rearrange("k (q i) -> k q i", i=QUARTER)[:, 0:3, 0 : 2 * CHUNKS]
        for j in range(2):
            nc.scalar.activation(size[:, j], used, ABS, bias=(0.0, -math.pi / 2)[j])
        nc.scalar.activation(factors[:], size[:], SIN, bias=math.pi / 2, scale=-1.0)
        first = factors[:, :, 2, 0:CHUNKS].rearrange("k b c -> k c b")
        later = factors[:, :, 0:2].rearrange("k j x (l c) -> k j x l c", c=CHUNKS)

        turned = held.tile([P, CHUNKS, 2, 2], F32, name="turned")
        for_both = [P, CHUNKS, 2, 2]
        nc.vector.tensor_tensor(
            turned[:], first.unsqueeze(2).broadcast_to(for_both), later[:, :, :, 0].rearrange("k a b c -> k c a b"), MULT
        )

        entries = held.tile([P, 2, CHUNKS, 2, 2], F32, name="entries")
        cosines, sines = (
            later[:, f, :, 1].rearrange("k a c -> k c a").unsqueeze(3).broadcast_to(for_both) for f in range(2)
        )
        nc.vector.tensor_tensor(entries[:, 0], turned[:], cosines, MULT)
        nc.vector.tensor_tensor(entries[:, 1], turned[:, :, :, ::-1], sines, MULT)

        matrix = held.tile([P, CHUNKS, 2, P], F32, name="matrix")
        def spread_out(c, products):
            spread = [P, products.stop - products.start, GROUPS, GROUP]
            nc.vector.tensor_tensor(
                matrix[:, c, products].rearrange("k t (g d) -> k t g d", d=GROUP),
                entries[:, products, c].rearrange("k t a b -> k t (a b)").unsqueeze(2).broadcast_to(spread),
                signed_group[:, products].rearrange("k t (g d) -> k t g d", d=GROUP),
                MULT,
            )

        for t in range(2):
            spread_out(0, slice(t, t + 1))
        for c in range(1, CHUNKS):
            spread_out(c, slice(0, 2))

        flipped = []

        def flip(r):
            flipped.append(in_turn.tile([P, N], F32, name="flipped", tag="turn"))
            for half in range(2):
                flipped_bank = banks.tile([P, 2, P], F32, name="flipped_bank", tag="bank")
                for e in range(2):
                    c = 2 * half + e
                    block = fresh[r][:, c * P : (c + 1) * P]
                    if 2 <= r * CHUNKS + c < 5:
                        nc.tensor.matmul(flipped_bank[:, e], lhsT=block, rhs=identity[:], start=True, stop=True)
                    else:
                        nc.tensor.transpose(flipped_bank[:, e], block, identity[:])
                nc.scalar.copy(
                    flipped[r][:, 2 * half * P : 2 * (half + 1) * P], flipped_bank[:].rearrange("k e j -> k (e j)")
                )

        for r in range(BLOCKS):
            if r % AHEAD == 0:
                for ahead in range(r, r + AHEAD):
                    flip(ahead)
            products = rows.tile([P, 2, N], F32, name="products")
            for c in range(CHUNKS):
                here = slice(c * P, (c + 1) * P)
                if r == 0 and c in (0, CHUNKS - 1):
                    for t, copy_out in enumerate((nc.vector.tensor_copy, nc.scalar.copy)):
                        half_bank = banks.tile([P, P], F32, name="half_bank", tag="bank")
                        nc.tensor.matmul(half_bank[:], lhsT=flipped[r][:, here], rhs=matrix[:, c, t], start=True, stop=True)
                        copy_out(products[:, t, here], half_bank[:])
                else:
                    bank = banks.tile([P, 2, P], F32, name="bank", tag="bank")
                    nc.tensor.matmul(bank[:], lhsT=flipped[r][:, here], rhs=matrix[:, c], start=True, stop=True)
                    copy_out = nc.vector.tensor_copy if r == 0 and c % 2 else nc.scalar.copy
                    copy_out(products[:, :, here], bank[:])

            nc.vector.tensor_tensor(windows[r][:].indirect(offsets[:]), products[:, 0], products[:, 1], ADD)
            nc.sync.dma_start(out[r * P : (r + 1) * P, :], windows[r][:])
